import numpy as np
import ml_dtypes


def mxq(x, axis, fmt="e4m3"):
    dtype, down = {"e4m3": (ml_dtypes.float8_e4m3fn, 7), "e5m2": (ml_dtypes.float8_e5m2, 14)}[fmt]
    v = np.moveaxis(np.asarray(x, np.float32).astype(ml_dtypes.bfloat16).astype(np.float64), axis, -1)
    blocks = v.reshape(v.shape[:-1] + (-1, 32))
    amax = np.abs(blocks).max(-1, keepdims=True)
    byte = np.maximum(np.where(amax > 0, np.frexp(amax)[1] - 1 + 127, 0) - down, 1)
    scale = np.exp2(byte - 127.0)
    codes = (blocks / scale).astype(np.float32).astype(dtype).astype(np.float64)
    return np.moveaxis((codes * scale).reshape(v.shape), -1, axis)


WIDE = False


def mx_kscale(k):
    if not WIDE:
        return np.ones(k)
    levels = np.array([10, -10, 5, -5, 0])
    if k % 512:
        return np.exp2(np.random.permutation(np.resize(levels, k // 32))).repeat(32)
    a = np.empty((k // 512, 16))
    for p in range(k // 512):
        a[p, :8] = np.random.permutation(np.resize(levels, 8))
        for g in range(8):
            far = levels[np.abs(levels - a[p, g]) >= 10]
            a[p, g + 8] = far[np.random.randint(len(far))]
    return np.exp2(a.ravel()).repeat(32)


BF16 = ml_dtypes.bfloat16


def bf(x):
    return np.asarray(x, np.float32).astype(BF16)


def f64(x):
    return np.asarray(x).astype(np.float64)


E2M1 = np.array([0.0, 0.5, 1.0, 1.5, 2.0, 3.0, 4.0, 6.0, -0.0, -0.5, -1.0, -1.5, -2.0, -3.0, -4.0, -6.0])


def pack_weight(w, fmt):
    k, n = w.shape
    w = f64(bf(w)).reshape(k // 32, 32, n)
    amax = np.abs(w).max(1)
    if fmt == "e4m3":
        byte = np.frexp(amax)[1] - 1 + 127 - 7
    else:
        mant, ex = np.frexp(amax / 6.0)
        byte = np.where(mant > 0.5, ex, ex - 1) + 127
    byte = np.clip(np.where(amax > 0, byte, 1), 1, 254)
    scaled = (w * np.exp2(127.0 - byte)[:, None, :]).reshape(k, n).astype(np.float32)
    by_word = np.ascontiguousarray(scaled.reshape(k // 512, 128, 4, n).transpose(0, 1, 3, 2))
    if fmt == "e4m3":
        words = by_word.astype(ml_dtypes.float8_e4m3fn).view(np.uint8)
    else:
        c = by_word.astype(ml_dtypes.float4_e2m1fn).view(np.uint8) & 0xF
        words = c[..., 0::2] | (c[..., 1::2] << 4)
    return np.ascontiguousarray(words), np.ascontiguousarray(byte.astype(np.uint8).reshape(k // 512, 16, n))


def unpack_weight(words, scales, fmt):
    g, p, n, _ = words.shape
    if fmt == "e4m3":
        vals = np.ascontiguousarray(words).view(ml_dtypes.float8_e4m3fn).astype(np.float64)
    else:
        nib = np.empty((g, p, n, 4), np.uint8)
        nib[..., 0::2] = words & 0xF
        nib[..., 1::2] = words >> 4
        vals = E2M1[nib]
    vals = vals * np.repeat(np.exp2(scales.astype(np.float64) - 127.0), 8, axis=1)[..., None]
    return vals.transpose(0, 1, 3, 2).reshape(g * 512, n)


B, S, HIDDEN, Q_LORA, NUM_HEADS, QK_NOPE, QK_ROPE, KV_LORA = 2, 256, 2048, 1536, 16, 128, 64, 448
QK_HEAD = QK_NOPE + QK_ROPE


def rotate_half(t):
    d = t.shape[-1] // 2
    return np.concatenate([-t[..., d:], t[..., :d]], axis=-1)


def draw0():
    s, t = mx_kscale(HIDDEN), mx_kscale(Q_LORA)
    x = bf(np.random.standard_normal((B, S, HIDDEN)) * s)
    cos = bf(np.random.uniform(size=(B, S, QK_ROPE)))
    sin = bf(np.random.uniform(size=(B, S, QK_ROPE)))
    Wqa = np.random.standard_normal((Q_LORA, HIDDEN)) / np.sqrt(HIDDEN) * t[:, None] / s
    Wqb = np.random.standard_normal((NUM_HEADS * QK_HEAD, Q_LORA)) / np.sqrt(Q_LORA) / t
    Wkva = np.random.standard_normal((KV_LORA + QK_ROPE, HIDDEN)) / np.sqrt(HIDDEN) / s
    Wqa_words, Wqa_scales = pack_weight(Wqa.T, "e4m3")
    Wqb_words, Wqb_scales = pack_weight(Wqb.T, "e4m3")
    Wkva_words, Wkva_scales = pack_weight(Wkva.T, "e4m3")
    return {"x": x, "cos": cos, "sin": sin, "Wqa_words": Wqa_words, "Wqa_scales": Wqa_scales, "Wqb_words": Wqb_words, "Wqb_scales": Wqb_scales, "Wkva_words": Wkva_words, "Wkva_scales": Wkva_scales}


def core(x, cos, sin, Wqa_words, Wqa_scales, Wqb_words, Wqb_scales, Wkva_words, Wkva_scales):
    b, s, _ = x.shape
    xq = mxq(f64(x), 2, "e4m3")
    qa = xq @ unpack_weight(Wqa_words, Wqa_scales, "e4m3")
    q = (mxq(qa, 2, "e4m3") @ unpack_weight(Wqb_words, Wqb_scales, "e4m3")).reshape(b, s, NUM_HEADS, QK_HEAD)
    q_nope = q[..., :QK_NOPE]
    q_pe = q[..., QK_NOPE:]
    kv = xq @ unpack_weight(Wkva_words, Wkva_scales, "e4m3")
    compressed_kv = kv[..., :KV_LORA]
    k_pe = kv[..., KV_LORA:].reshape(b, s, 1, QK_ROPE)
    c = f64(cos)[:, :, None, :]
    sn = f64(sin)[:, :, None, :]
    q_pe_rot = q_pe * c + rotate_half(q_pe) * sn
    k_pe_rot = k_pe * c + rotate_half(k_pe) * sn
    q_out = np.concatenate([q_nope, q_pe_rot], axis=-1).reshape(b, s, -1)
    k_out = k_pe_rot.reshape(b, s, QK_ROPE)
    return np.concatenate([q_out, k_out, compressed_kv], axis=-1)


def e4m3fn_bytes(y):
    return np.clip(np.asarray(y, np.float64), -448.0, 448.0).astype(np.float32).astype(ml_dtypes.float8_e4m3fn).view(np.uint8)


def e4m3fn_values(b):
    return np.asarray(b, np.uint8).view(ml_dtypes.float8_e4m3fn).astype(np.float64)


def setup_inputs():
    d = draw0()
    x0 = np.asarray(d['x']).astype(np.float64)
    s = (np.max(np.abs(x0), axis=(0, 1), keepdims=True) / 448.0).astype(np.float32)
    out = {}
    for k, v in d.items():
        if k == 'x':
            out['x_bytes'] = e4m3fn_bytes(x0 / s.astype(np.float64))
            out['x_scale'] = s
        else:
            out[k] = v
    return out


def reference(x_bytes, x_scale, cos, sin, Wqa_words, Wqa_scales, Wqb_words, Wqb_scales, Wkva_words, Wkva_scales):
    return core(e4m3fn_values(x_bytes) * x_scale.astype(np.float64), cos, sin, Wqa_words, Wqa_scales, Wqb_words, Wqb_scales, Wkva_words, Wkva_scales)

@@ -1,0 +1,396 @@
+from contextlib import ExitStack
+
+import concourse.mybir as mybir
+from concourse.masks import make_identity
+
+TOKENS, HIDDEN, Q_LORA = 512, 2048, 1536
+HEADS, NOPE, ROPE, KV_LORA = 16, 128, 64, 448
+HEAD = NOPE + ROPE
+Q_COLS = HEADS * HEAD
+KV_COLS = KV_LORA + ROPE
+
+FLOPS = 2 * TOKENS * HIDDEN * (Q_LORA + KV_COLS) + 2 * TOKENS * Q_LORA * Q_COLS
+
+F32 = mybir.dt.float32
+BF16 = mybir.dt.bfloat16
+I32 = mybir.dt.int32
+U32 = mybir.dt.uint32
+U8 = mybir.dt.uint8
+FP8 = mybir.dt.float8_e4m3fn
+FP8X4 = mybir.dt.float8_e4m3fn_x4
+MULT = mybir.AluOpType.mult
+ADD = mybir.AluOpType.add
+
+P = 128
+BANK = 512
+TILES = TOKENS // P
+XG = HIDDEN // 512
+QG = Q_LORA // 512
+HALF = Q_COLS // 2
+
+
+def tile_mlaselfattn_w8_kernel(
+    tc, x_bytes, x_scale, cos, sin, wqa_words, wqa_scales, wqb_words, wqb_scales, wkva_words, wkva_scales, out
+):
+    nc = tc.nc
+    x_rows = x_bytes.rearrange("b s k -> (b s) k")
+    out_rows = out.rearrange("b s c -> (b s) c")
+
+    with ExitStack() as ctx:
+        keep = ctx.enter_context(tc.tile_pool(name="keep", bufs=1))
+        work = ctx.enter_context(tc.tile_pool(name="work", bufs=2))
+        psum = ctx.enter_context(tc.psum_pool(name="psum", bufs=8))
+
+        def bank_tile():
+            return psum.tile([P, BANK], F32, name="bank")
+
+        def kept(name, shape, dtype):
+            return keep.tile(shape, dtype, name=name, align_bytes=64)
+
+        xb = [kept("xb%d" % i, [P, HIDDEN], U8) for i in range(TILES)]
+        xv = [kept("xv%d" % i, [P, HIDDEN], BF16) for i in range(TILES)]
+        xp = {i: kept("xp%d" % i, [P, XG, 2, P], F32) for i in (2, 3)}
+        xg = [kept("xg%d" % i, [P, XG, P, 4], BF16) for i in range(TILES)]
+        xc = [kept("xc%d" % i, [P, XG, P], U32) for i in range(TILES)]
+        xs = [kept("xs%d" % i, [P, XG, P], U8) for i in range(TILES)]
+        qv = [kept("qv%d" % i, [P, QG, BANK], BF16) for i in range(TILES)]
+        qg = [kept("qg%d" % i, [P, QG, P, 4], BF16) for i in range(TILES)]
+        qc = [kept("qc%d" % i, [P, QG, P], U32) for i in range(TILES)]
+        qs = [kept("qs%d" % i, [P, QG, P], U8) for i in range(TILES)]
+        wa = [kept("wa%d" % g, [P, Q_LORA], U32) for g in range(XG)]
+        wb = [kept("wb%d" % g, [P, Q_COLS], U32) for g in range(QG)]
+        wk = kept("wk", [P, XG, KV_COLS], U32)
+        sa = kept("sa", [P, Q_LORA], U8)
+        sb = kept("sb", [P, Q_COLS], U8)
+        sk = kept("sk", [P, KV_COLS], U8)
+        kscale = kept("kscale", [P, XG, 4], F32)
+        cos_sb = kept("cos_sb", [P, TILES, ROPE], BF16)
+        sin_sb = kept("sin_sb", [P, TILES, ROPE], BF16)
+        sin_neg = kept("sin_neg", [P, TILES, ROPE // 2], BF16)
+        ckv = [kept("ckv%d" % i, [P, KV_LORA], F32) for i in range(TILES)]
+        kp = kept("kp", [P, TILES, ROPE], F32)
+        kt = kept("kt", [P, TILES, ROPE], F32)
+        kt2 = kept("kt2", [P, TILES, ROPE], F32)
+        ident = kept("ident", [P, P], F32)
+        warm = kept("warm", [P, 8], F32)
+        zeros = kept("zeros", [P, P + BANK], BF16)
+
+        ctx.enter_context(tc.manual_schedule())
+
+        nc.vector.memset(warm[:], 0.0)
+        nc.vector.memset(zeros[:], 0.0)
+        nc.vector.memset(sa[:].bitcast(I32), 0)
+        nc.vector.memset(sk[:].bitcast(I32), 0)
+        nc.vector.memset(sb[:].bitcast(I32), 0)
+        make_identity(nc, ident[:])
+
+        def load_x(i):
+            nc.sync.dma_start(out=xb[i][:], in_=x_rows[i * P : (i + 1) * P, :])
+
+        def load_words(tile, words):
+            nc.sync.dma_start(out=tile.bitcast(I32), in_=words.rearrange("p n t -> p (n t)").bitcast(I32))
+
+        def load_planes(tile, scales):
+            groups = scales.shape[0]
+            for q in range(4):
+                nc.sync.dma_start(
+                    out=tile[32 * q : 32 * q + 4 * groups, :].bitcast(I32),
+                    in_=scales[:, 4 * q : 4 * q + 4, :].bitcast(I32),
+                )
+
+        load_x(0)
+        nc.scalar.dma_start(out=kscale[:], in_=x_scale.rearrange("a b (g p t) -> p (a b g) t", p=P, t=4))
+        nc.scalar.copy(out=warm[:, 4:8], in_=warm[:, 0:4])
+        load_planes(sa, wqa_scales)
+        load_x(1)
+        load_words(wa[0][:], wqa_words[0])
+        load_words(wa[1][:], wqa_words[1])
+        load_x(2)
+        load_words(wa[2][:], wqa_words[2])
+        load_x(3)
+        load_words(wa[3][:], wqa_words[3])
+        load_planes(sk, wkva_scales)
+        nc.sync.dma_start(
+            out=wk[:].bitcast(I32),
+            in_=wkva_words.rearrange("g p n t -> p g (n t)").bitcast(I32),
+        )
+        load_planes(sb, wqb_scales)
+        for h in range(2):
+            if h:
+                nc.sync.dma_start(out=cos_sb[:], in_=cos.rearrange("b (h p) d -> p (b h) d", p=P))
+                nc.sync.dma_start(out=sin_sb[:], in_=sin.rearrange("b (h p) d -> p (b h) d", p=P))
+            for g in range(QG):
+                cols = slice(HALF * h, HALF * (h + 1))
+                load_words(wb[g][:, cols], wqb_words[g, :, cols, :])
+
+        turned = {}
+        acc = {}
+
+        def cast(i, first, last, copy=nc.scalar.copy):
+            cols = slice(512 * first // 2, 512 * last // 2)
+            copy(out=xv[i][:, cols], in_=xb[i][:, cols].bitcast(FP8))
+
+        def spread(i, g, n):
+            words = xv[i][:, 512 * g : 512 * (g + n)].bitcast(F32)
+            nc.vector.tensor_copy(
+                out=xp[i][:, g : g + n, :, :], in_=words.rearrange("p (g q u) -> p g u q", g=n, u=2)
+            )
+
+        def turn(i, g, n):
+            bank = bank_tile()[:].rearrange("p (j u r) -> p j u r", j=2, u=2)
+            words = xv[i][:].bitcast(F32)
+            for j in range(n):
+                base = 256 * (g + j)
+                for u in range(2):
+                    source = xp[i][:, g + j, u, :] if i in xp else words[:, base + u : base + 256 : 2]
+                    nc.tensor.transpose(bank[:, j, u, :], source, ident[:])
+                turned[(i, g + j)] = bank[:, j, :, :]
+
+        def keep_warm(bank, n):
+            for j in range(n):
+                nc.tensor.matmul(bank[:], lhsT=zeros[:, 0:P], rhs=zeros[:, P:], start=True, stop=True)
+
+        def widen(i, g):
+            nc.vector.tensor_tensor(
+                out=xg[i][:, g, :, :].rearrange("p r (u e) -> p r u e", e=2),
+                in0=turned[(i, g)].bitcast(BF16).rearrange("p u (r e) -> p r u e", e=2),
+                in1=kscale[:, g, :].rearrange("p (u e) -> p u e", e=2).unsqueeze(1).to_broadcast([P, P, 2, 2]),
+                op=MULT,
+            )
+
+        def quant_x(i, g, n):
+            gs = slice(g, g + n)
+            nc.vector.quantize_mx(
+                out=xc[i][:, gs, :].rearrange("p g r -> p (g r)").bitcast(FP8X4),
+                scales=xs[i][:, gs, :].rearrange("p g r -> p (g r)"),
+                in_=xg[i][:, gs, :, :].rearrange("p g r t -> p (g r t)"),
+            )
+
+        def qa_pass(i, g, n):
+            if g == 0:
+                acc[(i, n)] = bank_tile()
+            cols = slice(BANK * n, BANK * (n + 1))
+            nc.tensor.matmul_mx(
+                out=acc[(i, n)][:],
+                lhsT=xc[i][:, g, :].bitcast(FP8X4),
+                lhsT_scale=xs[i][:, g, :],
+                rhs=wa[g][:, cols].bitcast(FP8X4),
+                rhs_scale=sa[4 * g : P, cols],
+                start=(g == 0),
+                stop=(g == XG - 1),
+            )
+
+        def qa_group(i, g):
+            for n in range(QG):
+                qa_pass(i, g, n)
+
+        def qa_bank(i, n):
+            for g in range(XG):
+                qa_pass(i, g, n)
+
+        def round_qa(i, n):
+            nc.scalar.copy(
+                out=qv[i][:, n, :].rearrange("p (u q e) -> p u q e", u=2, e=2),
+                in_=acc[(i, n)][:].rearrange("p (q u e) -> p u q e", u=2, e=2),
+            )
+
+        def turn_qa(i):
+            words = qv[i][:].rearrange("p g c -> p (g c)").bitcast(F32)
+            for first, n in ((0, 2), (2, 1)):
+                bank = bank_tile()[:].rearrange("p (j u r) -> p j u r", j=2, u=2)
+                for j in range(n):
+                    for u in range(2):
+                        base = 256 * (first + j) + P * u
+                        nc.tensor.transpose(bank[:, j, u, :], words[:, base : base + P], ident[:])
+                nc.scalar.copy(
+                    out=qg[i][:, first : first + n, :, :].rearrange("p g r t -> p (g r t)").bitcast(F32).rearrange("p (g r u) -> p g r u", g=n, u=2),
+                    in_=bank[:, 0:n, :, :].rearrange("p g u r -> p g r u"),
+                )
+
+        def quant_qa(i):
+            for first, n in ((0, 2), (2, 1)):
+                gs = slice(first, first + n)
+                nc.vector.quantize_mx(
+                    out=qc[i][:, gs, :].rearrange("p g r -> p (g r)").bitcast(FP8X4),
+                    scales=qs[i][:, gs, :].rearrange("p g r -> p (g r)"),
+                    in_=qg[i][:, gs, :, :].rearrange("p g r t -> p (g r t)"),
+                )
+
+        def kv(i, first, last):
+            bank = bank_tile()
+            for g in range(XG):
+                nc.tensor.matmul_mx(
+                    out=bank[:, first:last],
+                    lhsT=xc[i][:, g, :].bitcast(FP8X4),
+                    lhsT_scale=xs[i][:, g, :],
+                    rhs=wk[:, g, first:last].bitcast(FP8X4),
+                    rhs_scale=sk[4 * g : P, first:last],
+                    start=(g == 0),
+                    stop=(g == XG - 1),
+                )
+            acc[("kv", i, first)] = bank
+
+        def out_kv(i, first, last):
+            bank = acc[("kv", i, first)]
+            end = min(last, KV_LORA)
+            nc.scalar.copy(out=ckv[i][:, first:end], in_=bank[:, first:end])
+            if last > KV_LORA:
+                nc.scalar.copy(out=kp[:, i, :], in_=bank[:, KV_LORA:])
+            nc.scalar.dma_start(
+                out=out_rows[i * P : (i + 1) * P, Q_COLS + ROPE + first : Q_COLS + ROPE + end], in_=ckv[i][:, first:end]
+            )
+
+        def kv_part(i, first):
+            kv(i, first, first + 256)
+            out_kv(i, first, first + 256)
+
+        def rope_k(first, last):
+            rope(
+                kp[:, first:last, :],
+                cos_sb[:, first:last, :],
+                sin_neg[:, first:last, :],
+                sin_sb[:, first:last, ROPE // 2 :],
+                kt[:, first:last, :],
+                kt2[:, first:last, :],
+            )
+            nc.sync.dma_start(
+                out=out_rows[first * P : last * P, Q_COLS : Q_COLS + ROPE].rearrange("(i p) c -> p i c", p=P),
+                in_=kp[:, first:last, :],
+            )
+
+        def rope(pe, c, sn, s2, t1, t2):
+            h = ROPE // 2
+            nc.vector.tensor_tensor(out=t2[:, :, 0:h], in0=pe[:, :, h:], in1=sn, op=MULT)
+            nc.vector.tensor_tensor(out=t2[:, :, h:], in0=pe[:, :, 0:h], in1=s2, op=MULT)
+            nc.vector.tensor_tensor(out=t1, in0=pe, in1=c, op=MULT)
+            nc.vector.tensor_tensor(out=pe, in0=t1, in1=t2, op=ADD)
+
+        def rope_q(i, q, first):
+            pe = q[:].rearrange("p (b c) -> p b c", c=ROPE)[:, first::3, :]
+            h = pe.shape[1]
+            t1 = work.tile([P, 8, ROPE], F32, name="t1")
+            t2 = work.tile([P, 8, ROPE], F32, name="t2")
+            rope(
+                pe,
+                cos_sb[:, i, :].unsqueeze(1).to_broadcast([P, h, ROPE]),
+                sin_neg[:, i, :].unsqueeze(1).to_broadcast([P, h, ROPE // 2]),
+                sin_sb[:, i, ROPE // 2 :].unsqueeze(1).to_broadcast([P, h, ROPE // 2]),
+                t1[:, 0:h, :],
+                t2[:, 0:h, :],
+            )
+
+        def q_bank(i, n):
+            bank = bank_tile()
+            cols = slice(BANK * n, BANK * (n + 1))
+            for g in range(QG):
+                nc.tensor.matmul_mx(
+                    out=bank[:],
+                    lhsT=qc[i][:, g, :].bitcast(FP8X4),
+                    lhsT_scale=qs[i][:, g, :],
+                    rhs=wb[g][:, cols].bitcast(FP8X4),
+                    rhs_scale=sb[4 * g : P, cols],
+                    start=(g == 0),
+                    stop=(g == QG - 1),
+                )
+            return bank
+
+        def q_part(i, first, n):
+            q = work.tile([P, n * BANK], F32, name="q%d" % n, bufs=4)
+            for j in range(n):
+                bank = q_bank(i, first + j)
+                nc.scalar.copy(out=q[:, BANK * j : BANK * (j + 1)], in_=bank[:])
+            rope_q(i, q, (2 - 8 * first) % 3)
+            nc.sync.dma_start(out=out_rows[i * P : (i + 1) * P, BANK * first : BANK * (first + n)], in_=q[:])
+
+        idle = bank_tile()
+        keep_warm(idle, 5)
+        cast(0, 0, 1)
+        cast(0, 1, 2, nc.vector.tensor_copy)
+        cast(0, 2, 4)
+        cast(0, 4, 6, nc.vector.tensor_copy)
+        cast(0, 6, 8)
+        for g in range(XG):
+            turn(0, g, 1)
+            if g < 2:
+                keep_warm(idle, 1)
+            widen(0, g)
+            if g:
+                quant_x(0, g - 1, 1)
+        cast(1, 0, 4)
+        cast(1, 4, 8)
+        turn(1, 0, 2)
+        qa_group(0, 0)
+        widen(1, 0)
+        quant_x(0, 3, 1)
+        widen(1, 1)
+        quant_x(1, 0, 1)
+        turn(1, 2, 2)
+        cast(2, 0, 4)
+        widen(1, 2)
+        quant_x(1, 1, 1)
+        cast(2, 4, 8)
+        qa_group(0, 1)
+        qa_group(1, 0)
+        widen(1, 3)
+        spread(2, 0, 2)
+        quant_x(1, 2, 2)
+        spread(2, 2, 2)
+        qa_group(1, 1)
+        qa_group(0, 2)
+        turn(2, 0, 2)
+        turn(2, 2, 2)
+        widen(2, 0)
+        widen(2, 1)
+        cast(3, 0, 4)
+        cast(3, 4, 8)
+        qa_group(1, 2)
+        qa_group(0, 3)
+        spread(3, 0, 2)
+        widen(2, 2)
+        spread(3, 2, 2)
+        quant_x(2, 0, 2)
+        widen(2, 3)
+        quant_x(2, 2, 2)
+        for n in range(QG):
+            round_qa(0, n)
+        qa_group(1, 3)
+        turn(3, 0, 2)
+        turn(3, 2, 2)
+        for n in range(QG):
+            round_qa(1, n)
+        widen(3, 0)
+        widen(3, 1)
+        for g in range(XG):
+            qa_group(2, g)
+        widen(3, 2)
+        quant_x(3, 0, 2)
+        widen(3, 3)
+        turn_qa(0)
+        quant_x(3, 2, 2)
+        turn_qa(1)
+        quant_qa(0)
+        quant_qa(1)
+        for n in range(QG):
+            round_qa(2, n)
+        nc.vector.tensor_scalar(out=sin_neg[:], in0=sin_sb[:, :, 0 : ROPE // 2], scalar1=-1.0, scalar2=None, op0=MULT)
+        for n in range(QG):
+            qa_bank(3, n)
+        for n in range(QG):
+            round_qa(3, n)
+        q_part(0, 0, 3)
+        q_part(1, 0, 3)
+        turn_qa(2)
+        quant_qa(2)
+        turn_qa(3)
+        quant_qa(3)
+        q_part(0, 3, 3)
+        q_part(1, 3, 3)
+        q_part(2, 0, 3)
+        q_part(2, 3, 3)
+        q_part(3, 0, 3)
+        q_part(3, 3, 3)
+        for i in range(TILES):
+            kv_part(i, 256)
+        rope_k(0, 4)
+        for i in range(TILES):
+            kv_part(i, 0)

@@ -26,30 +26,30 @@ BANK = 512
 TILES = TOKENS // P
 XG = HIDDEN // 512
 QG = Q_LORA // 512
-HALF = Q_COLS // 2
+HALF = BANK // 2
 
 
 def tile_mlaselfattn_w8_kernel(
     tc, x_bytes, x_scale, cos, sin, wqa_words, wqa_scales, wqb_words, wqb_scales, wkva_words, wkva_scales, out
 ):
     nc = tc.nc
-    x_rows = x_bytes.rearrange("b s k -> (b s) k")
-    out_rows = out.rearrange("b s c -> (b s) c")
+    x_rows = x_bytes.rearrange("b (q i) k -> (b q) i k", i=TILES)
+    out_rows = out.rearrange("b (q i) c -> (b q) i c", i=TILES)
 
     with ExitStack() as ctx:
         keep = ctx.enter_context(tc.tile_pool(name="keep", bufs=1))
         work = ctx.enter_context(tc.tile_pool(name="work", bufs=2))
-        psum = ctx.enter_context(tc.psum_pool(name="psum", bufs=8))
+        psum = ctx.enter_context(tc.psum_pool(name="psum", bufs=1))
 
-        def bank_tile():
-            return psum.tile([P, BANK], F32, name="bank")
+        def bank_tile(b):
+            return psum.tile([P, BANK], F32, name="bank%d" % b)
 
         def kept(name, shape, dtype):
             return keep.tile(shape, dtype, name=name, align_bytes=64)
 
-        xb = [kept("xb%d" % i, [P, HIDDEN], U8) for i in range(TILES)]
-        xv = [kept("xv%d" % i, [P, HIDDEN], BF16) for i in range(TILES)]
-        xp = {i: kept("xp%d" % i, [P, XG, 2, P], F32) for i in (2, 3)}
+        xb_pair = [kept("xb_pair%d" % h, [P, 2, HIDDEN // 2], U8) for h in range(2)]
+        xb_tile = {i: kept("xb_tile%d" % i, [P, HIDDEN], U8) for i in (2, 3)}
+        xv = {(i, g): kept("xv%d_%d" % (i, g), [P, 512], BF16) for i in range(TILES) for g in range(XG)}
         xg = [kept("xg%d" % i, [P, XG, P, 4], BF16) for i in range(TILES)]
         xc = [kept("xc%d" % i, [P, XG, P], U32) for i in range(TILES)]
         xs = [kept("xs%d" % i, [P, XG, P], U8) for i in range(TILES)]
@@ -57,8 +57,9 @@ def tile_mlaselfattn_w8_kernel(
         qg = [kept("qg%d" % i, [P, QG, P, 4], BF16) for i in range(TILES)]
         qc = [kept("qc%d" % i, [P, QG, P], U32) for i in range(TILES)]
         qs = [kept("qs%d" % i, [P, QG, P], U8) for i in range(TILES)]
-        wa = [kept("wa%d" % g, [P, Q_LORA], U32) for g in range(XG)]
-        wb = [kept("wb%d" % g, [P, Q_COLS], U32) for g in range(QG)]
+        wa0 = [kept("wa0_%d" % n, [P, BANK], U32) for n in range(QG)]
+        wa = {g: kept("wa%d" % g, [P, Q_LORA], U32) for g in range(1, XG)}
+        wb = [kept("wb%d" % c, [P, QG, 2 * BANK], U32) for c in range(3)]
         wk = kept("wk", [P, XG, KV_COLS], U32)
         sa = kept("sa", [P, Q_LORA], U8)
         sb = kept("sb", [P, Q_COLS], U8)
@@ -67,28 +68,34 @@ def tile_mlaselfattn_w8_kernel(
         cos_sb = kept("cos_sb", [P, TILES, ROPE], BF16)
         sin_sb = kept("sin_sb", [P, TILES, ROPE], BF16)
         sin_neg = kept("sin_neg", [P, TILES, ROPE // 2], BF16)
-        ckv = [kept("ckv%d" % i, [P, KV_LORA], F32) for i in range(TILES)]
-        kp = kept("kp", [P, TILES, ROPE], F32)
-        kt = kept("kt", [P, TILES, ROPE], F32)
-        kt2 = kept("kt2", [P, TILES, ROPE], F32)
+        sk_raw = kept("sk_raw", [P, KV_COLS], U8)
+        xw = {(i, g): kept("xw%d_%d" % (i, g), [P, 2, P], F32) for i in range(TILES) for g in range(XG)}
+        one = kept("one", [P, 8], F32)
         ident = kept("ident", [P, P], F32)
         warm = kept("warm", [P, 8], F32)
-        zeros = kept("zeros", [P, P + BANK], BF16)
+        zeros = kept("zeros", [P, BANK], BF16)
 
         ctx.enter_context(tc.manual_schedule())
 
-        nc.vector.memset(warm[:], 0.0)
-        nc.vector.memset(zeros[:], 0.0)
         nc.vector.memset(sa[:].bitcast(I32), 0)
-        nc.vector.memset(sk[:].bitcast(I32), 0)
+        nc.vector.memset(zeros[:].bitcast(I32), 0)
+        nc.vector.memset(warm[:], 0.0)
+        nc.vector.memset(one[:], 1.0)
         nc.vector.memset(sb[:].bitcast(I32), 0)
+        nc.vector.memset(sk_raw[:].bitcast(I32), 0)
         make_identity(nc, ident[:])
 
+        def load_pair(h):
+            nc.sync.dma_start(out=xb_pair[h][:], in_=x_rows[:, 0:2, 1024 * h : 1024 * (h + 1)])
+
         def load_x(i):
-            nc.sync.dma_start(out=xb[i][:], in_=x_rows[i * P : (i + 1) * P, :])
+            nc.sync.dma_start(out=xb_tile[i][:], in_=x_rows[:, i, :])
 
         def load_words(tile, words):
             nc.sync.dma_start(out=tile.bitcast(I32), in_=words.rearrange("p n t -> p (n t)").bitcast(I32))
+
+        def load_groups(tile, words):
+            nc.sync.dma_start(out=tile.bitcast(I32), in_=words.rearrange("g p n t -> p g (n t)").bitcast(I32))
 
         def load_planes(tile, scales):
             groups = scales.shape[0]
@@ -98,57 +105,67 @@ def tile_mlaselfattn_w8_kernel(
                     in_=scales[:, 4 * q : 4 * q + 4, :].bitcast(I32),
                 )
 
-        load_x(0)
+        load_pair(0)
         nc.scalar.dma_start(out=kscale[:], in_=x_scale.rearrange("a b (g p t) -> p (a b g) t", p=P, t=4))
         nc.scalar.copy(out=warm[:, 4:8], in_=warm[:, 0:4])
         load_planes(sa, wqa_scales)
-        load_x(1)
-        load_words(wa[0][:], wqa_words[0])
-        load_words(wa[1][:], wqa_words[1])
+        for n in range(QG):
+            load_words(wa0[n][:], wqa_words[0, :, BANK * n : BANK * (n + 1), :])
+            if n == 0:
+                load_pair(1)
         load_x(2)
+        load_words(wa[1][:], wqa_words[1])
         load_words(wa[2][:], wqa_words[2])
         load_x(3)
         load_words(wa[3][:], wqa_words[3])
-        load_planes(sk, wkva_scales)
-        nc.sync.dma_start(
-            out=wk[:].bitcast(I32),
-            in_=wkva_words.rearrange("g p n t -> p g (n t)").bitcast(I32),
-        )
         load_planes(sb, wqb_scales)
-        for h in range(2):
-            if h:
-                nc.sync.dma_start(out=cos_sb[:], in_=cos.rearrange("b (h p) d -> p (b h) d", p=P))
-                nc.sync.dma_start(out=sin_sb[:], in_=sin.rearrange("b (h p) d -> p (b h) d", p=P))
-            for g in range(QG):
-                cols = slice(HALF * h, HALF * (h + 1))
-                load_words(wb[g][:, cols], wqb_words[g, :, cols, :])
+        load_groups(wb[0][:], wqb_words[:, :, 0 : 2 * BANK, :])
+        nc.sync.dma_start(out=cos_sb[:], in_=cos.rearrange("b (q i) d -> (b q) i d", i=TILES))
+        nc.sync.dma_start(out=sin_sb[:], in_=sin.rearrange("b (q i) d -> (b q) i d", i=TILES))
+        for c in range(1, 3):
+            load_groups(wb[c][:], wqb_words[:, :, 2 * BANK * c : 2 * BANK * (c + 1), :])
+        load_planes(sk_raw, wkva_scales)
+        load_groups(wk[:, :, 0:ROPE], wkva_words[:, :, KV_LORA:, :])
+        load_groups(wk[:, :, ROPE:], wkva_words[:, :, 0:KV_LORA, :])
 
         turned = {}
         acc = {}
 
-        def cast(i, first, last, copy=nc.scalar.copy):
-            cols = slice(512 * first // 2, 512 * last // 2)
-            copy(out=xv[i][:, cols], in_=xb[i][:, cols].bitcast(FP8))
+        sorted_units = set()
 
-        def spread(i, g, n):
-            words = xv[i][:, 512 * g : 512 * (g + n)].bitcast(F32)
-            nc.vector.tensor_copy(
-                out=xp[i][:, g : g + n, :, :], in_=words.rearrange("p (g q u) -> p g u q", g=n, u=2)
+        def codes_of(i, g):
+            if i < 2:
+                return xb_pair[g // 2][:, i, 512 * (g % 2) : 512 * (g % 2 + 1)].bitcast(FP8)
+            return xb_tile[i][:, 512 * g : 512 * (g + 1)].bitcast(FP8)
+
+        def cast(i, g):
+            nc.scalar.copy(out=xv[(i, g)][:], in_=codes_of(i, g))
+
+        def cast_sorted(i, g):
+            nc.vector.tensor_scalar(
+                out=xw[(i, g)][:].bitcast(BF16).rearrange("p u (q e) -> p q u e", e=2),
+                in0=codes_of(i, g).rearrange("p (q u e) -> p q u e", u=2, e=2),
+                scalar1=one[:, 0:1],
+                scalar2=None,
+                op0=MULT,
             )
+            sorted_units.add((i, g))
 
-        def turn(i, g, n):
-            bank = bank_tile()[:].rearrange("p (j u r) -> p j u r", j=2, u=2)
-            words = xv[i][:].bitcast(F32)
-            for j in range(n):
-                base = 256 * (g + j)
+        def sort(i, g):
+            nc.scalar.copy(out=xw[(i, g)][:], in_=xv[(i, g)][:].bitcast(F32).rearrange("p (q u) -> p u q", u=2))
+            sorted_units.add((i, g))
+
+        def turn(b, units):
+            bank = bank_tile(b)[:].rearrange("p (j u r) -> p j u r", j=2, u=2)
+            for j, unit in enumerate(units):
                 for u in range(2):
-                    source = xp[i][:, g + j, u, :] if i in xp else words[:, base + u : base + 256 : 2]
-                    nc.tensor.transpose(bank[:, j, u, :], source, ident[:])
-                turned[(i, g + j)] = bank[:, j, :, :]
+                    words = xw[unit][:, u, :] if unit in sorted_units else xv[unit][:].bitcast(F32)[:, u:256:2]
+                    nc.tensor.transpose(bank[:, j, u, :], words, ident[:])
+                turned[unit] = bank[:, j, :, :]
 
         def keep_warm(bank, n):
             for j in range(n):
-                nc.tensor.matmul(bank[:], lhsT=zeros[:, 0:P], rhs=zeros[:, P:], start=True, stop=True)
+                nc.tensor.matmul(bank[:], lhsT=zeros[:, 0:P], rhs=zeros[:], start=True, stop=True)
 
         def widen(i, g):
             nc.vector.tensor_tensor(
@@ -166,15 +183,16 @@ def tile_mlaselfattn_w8_kernel(
                 in_=xg[i][:, gs, :, :].rearrange("p g r t -> p (g r t)"),
             )
 
-        def qa_pass(i, g, n):
+        def qa_pass(i, g, n, b):
             if g == 0:
-                acc[(i, n)] = bank_tile()
+                acc[(i, n)] = bank_tile(b)
             cols = slice(BANK * n, BANK * (n + 1))
+            words = wa[g][:, cols] if g else wa0[n][:]
             nc.tensor.matmul_mx(
                 out=acc[(i, n)][:],
                 lhsT=xc[i][:, g, :].bitcast(FP8X4),
                 lhsT_scale=xs[i][:, g, :],
-                rhs=wa[g][:, cols].bitcast(FP8X4),
+                rhs=words.bitcast(FP8X4),
                 rhs_scale=sa[4 * g : P, cols],
                 start=(g == 0),
                 stop=(g == XG - 1),
@@ -182,11 +200,11 @@ def tile_mlaselfattn_w8_kernel(
 
         def qa_group(i, g):
             for n in range(QG):
-                qa_pass(i, g, n)
+                qa_pass(i, g, n, QG * i + n)
 
-        def qa_bank(i, n):
+        def qa_bank(i, n, b):
             for g in range(XG):
-                qa_pass(i, g, n)
+                qa_pass(i, g, n, b)
 
         def round_qa(i, n):
             nc.scalar.copy(
@@ -194,203 +212,235 @@ def tile_mlaselfattn_w8_kernel(
                 in_=acc[(i, n)][:].rearrange("p (q u e) -> p u q e", u=2, e=2),
             )
 
-        def turn_qa(i):
-            words = qv[i][:].rearrange("p g c -> p (g c)").bitcast(F32)
-            for first, n in ((0, 2), (2, 1)):
-                bank = bank_tile()[:].rearrange("p (j u r) -> p j u r", j=2, u=2)
-                for j in range(n):
-                    for u in range(2):
-                        base = 256 * (first + j) + P * u
-                        nc.tensor.transpose(bank[:, j, u, :], words[:, base : base + P], ident[:])
-                nc.scalar.copy(
-                    out=qg[i][:, first : first + n, :, :].rearrange("p g r t -> p (g r t)").bitcast(F32).rearrange("p (g r u) -> p g r u", g=n, u=2),
-                    in_=bank[:, 0:n, :, :].rearrange("p g u r -> p g r u"),
-                )
+        def turn_qa(b, units):
+            bank = bank_tile(b)[:].rearrange("p (j u r) -> p j u r", j=2, u=2)
+            for j, (i, g) in enumerate(units):
+                words = qv[i][:, g, :].bitcast(F32)
+                for u in range(2):
+                    nc.tensor.transpose(bank[:, j, u, :], words[:, P * u : P * (u + 1)], ident[:])
+                turned[("qa", i, g)] = bank[:, j, :, :]
 
-        def quant_qa(i):
-            for first, n in ((0, 2), (2, 1)):
-                gs = slice(first, first + n)
-                nc.vector.quantize_mx(
-                    out=qc[i][:, gs, :].rearrange("p g r -> p (g r)").bitcast(FP8X4),
-                    scales=qs[i][:, gs, :].rearrange("p g r -> p (g r)"),
-                    in_=qg[i][:, gs, :, :].rearrange("p g r t -> p (g r t)"),
-                )
+        def gather_qa(i, g):
+            nc.scalar.copy(
+                out=qg[i][:, g, :, :].rearrange("p r t -> p (r t)").bitcast(F32).rearrange("p (r u) -> p r u", u=2),
+                in_=turned[("qa", i, g)].rearrange("p u r -> p r u"),
+            )
 
-        def kv(i, first, last):
-            bank = bank_tile()
+        def quant_qa(i, g, n):
+            gs = slice(g, g + n)
+            nc.vector.quantize_mx(
+                out=qc[i][:, gs, :].rearrange("p g r -> p (g r)").bitcast(FP8X4),
+                scales=qs[i][:, gs, :].rearrange("p g r -> p (g r)"),
+                in_=qg[i][:, gs, :, :].rearrange("p g r t -> p (g r t)"),
+            )
+
+        def kv_group(i, first, target):
             for g in range(XG):
                 nc.tensor.matmul_mx(
-                    out=bank[:, first:last],
+                    out=target,
                     lhsT=xc[i][:, g, :].bitcast(FP8X4),
                     lhsT_scale=xs[i][:, g, :],
-                    rhs=wk[:, g, first:last].bitcast(FP8X4),
-                    rhs_scale=sk[4 * g : P, first:last],
+                    rhs=wk[:, g, first : first + HALF].bitcast(FP8X4),
+                    rhs_scale=sk[4 * g : P, first : first + HALF],
                     start=(g == 0),
                     stop=(g == XG - 1),
                 )
-            acc[("kv", i, first)] = bank
 
-        def out_kv(i, first, last):
-            bank = acc[("kv", i, first)]
-            end = min(last, KV_LORA)
-            nc.scalar.copy(out=ckv[i][:, first:end], in_=bank[:, first:end])
-            if last > KV_LORA:
-                nc.scalar.copy(out=kp[:, i, :], in_=bank[:, KV_LORA:])
-            nc.scalar.dma_start(
-                out=out_rows[i * P : (i + 1) * P, Q_COLS + ROPE + first : Q_COLS + ROPE + end], in_=ckv[i][:, first:end]
-            )
+        def order_kv_scales():
+            nc.vector.tensor_copy(out=sk[:, 0:ROPE].bitcast(I32), in_=sk_raw[:, KV_LORA:].bitcast(I32))
+            nc.vector.tensor_copy(out=sk[:, ROPE:].bitcast(I32), in_=sk_raw[:, 0:KV_LORA].bitcast(I32))
 
-        def kv_part(i, first):
-            kv(i, first, first + 256)
-            out_kv(i, first, first + 256)
-
-        def rope_k(first, last):
-            rope(
-                kp[:, first:last, :],
-                cos_sb[:, first:last, :],
-                sin_neg[:, first:last, :],
-                sin_sb[:, first:last, ROPE // 2 :],
-                kt[:, first:last, :],
-                kt2[:, first:last, :],
-            )
-            nc.sync.dma_start(
-                out=out_rows[first * P : last * P, Q_COLS : Q_COLS + ROPE].rearrange("(i p) c -> p i c", p=P),
-                in_=kp[:, first:last, :],
-            )
-
-        def rope(pe, c, sn, s2, t1, t2):
+        def rope_terms(t1, t2, pe, c, sn, s2):
             h = ROPE // 2
             nc.vector.tensor_tensor(out=t2[:, :, 0:h], in0=pe[:, :, h:], in1=sn, op=MULT)
             nc.vector.tensor_tensor(out=t2[:, :, h:], in0=pe[:, :, 0:h], in1=s2, op=MULT)
             nc.vector.tensor_tensor(out=t1, in0=pe, in1=c, op=MULT)
-            nc.vector.tensor_tensor(out=pe, in0=t1, in1=t2, op=ADD)
 
-        def rope_q(i, q, first):
-            pe = q[:].rearrange("p (b c) -> p b c", c=ROPE)[:, first::3, :]
-            h = pe.shape[1]
-            t1 = work.tile([P, 8, ROPE], F32, name="t1")
-            t2 = work.tile([P, 8, ROPE], F32, name="t2")
-            rope(
-                pe,
-                cos_sb[:, i, :].unsqueeze(1).to_broadcast([P, h, ROPE]),
-                sin_neg[:, i, :].unsqueeze(1).to_broadcast([P, h, ROPE // 2]),
-                sin_sb[:, i, ROPE // 2 :].unsqueeze(1).to_broadcast([P, h, ROPE // 2]),
-                t1[:, 0:h, :],
-                t2[:, 0:h, :],
+        def kv_fronts(b, first):
+            bank = bank_tile(b)[:].rearrange("p (j c) -> p j c", j=2)
+            tiles = slice(first, first + 2)
+            for j in range(2):
+                kv_group(first + j, 0, bank[:, j, :])
+            front = work.tile([P, 2, HALF], F32, name="front")
+            t1 = work.tile([P, 6, ROPE], F32, name="t1")
+            t2 = work.tile([P, 6, ROPE], F32, name="t2")
+            rope_terms(
+                t1[:, 0:2, :], t2[:, 0:2, :], bank[:, :, 0:ROPE], cos_sb[:, tiles, :], sin_neg[:, tiles, :], sin_sb[:, tiles, ROPE // 2 :]
             )
+            nc.vector.tensor_tensor(out=front[:, :, 0:ROPE], in0=t1[:, 0:2, :], in1=t2[:, 0:2, :], op=ADD)
+            nc.scalar.copy(out=front[:, :, ROPE:], in_=bank[:, :, ROPE:])
+            nc.sync.dma_start(out=out_rows[:, tiles, Q_COLS : Q_COLS + HALF], in_=front[:])
 
-        def q_bank(i, n):
-            bank = bank_tile()
+        def kv_back(b, i):
+            bank = bank_tile(b)
+            kv_group(i, HALF, bank[:, 0:HALF])
+            back = work.tile([P, HALF], F32, name="back", bufs=4)
+            nc.scalar.copy(out=back[:], in_=bank[:, 0:HALF])
+            nc.sync.dma_start(out=out_rows[:, i, Q_COLS + HALF :], in_=back[:])
+
+        def q_bank(i, n, b):
+            bank = bank_tile(b)
             cols = slice(BANK * n, BANK * (n + 1))
             for g in range(QG):
                 nc.tensor.matmul_mx(
                     out=bank[:],
                     lhsT=qc[i][:, g, :].bitcast(FP8X4),
                     lhsT_scale=qs[i][:, g, :],
-                    rhs=wb[g][:, cols].bitcast(FP8X4),
+                    rhs=wb[n // 2][:, g, BANK * (n % 2) : BANK * (n % 2 + 1)].bitcast(FP8X4),
                     rhs_scale=sb[4 * g : P, cols],
                     start=(g == 0),
                     stop=(g == QG - 1),
                 )
             return bank
 
-        def q_part(i, first, n):
-            q = work.tile([P, n * BANK], F32, name="q%d" % n, bufs=4)
-            for j in range(n):
-                bank = q_bank(i, first + j)
-                nc.scalar.copy(out=q[:, BANK * j : BANK * (j + 1)], in_=bank[:])
-            rope_q(i, q, (2 - 8 * first) % 3)
-            nc.sync.dma_start(out=out_rows[i * P : (i + 1) * P, BANK * first : BANK * (first + n)], in_=q[:])
+        def q_part(i, first, banks):
+            n = len(banks)
+            q = work.tile([P, n, BANK], F32, name="q%d" % n, bufs=6)
+            t1 = work.tile([P, 6, ROPE], F32, name="t1")
+            t2 = work.tile([P, 6, ROPE], F32, name="t2")
+            done = 0
+            for j, b in enumerate(banks):
+                bank = q_bank(i, first + j, b)[:].rearrange("p (b c) -> p b c", c=ROPE)
+                blocks = q[:, j, :].rearrange("p (b c) -> p b c", c=ROPE)
+                turning = (2 - 8 * (first + j)) % 3
+                h = len(range(turning, 8, 3))
+                rope_terms(
+                    t1[:, done : done + h, :],
+                    t2[:, done : done + h, :],
+                    bank[:, turning::3, :],
+                    cos_sb[:, i, :].unsqueeze(1).to_broadcast([P, h, ROPE]),
+                    sin_neg[:, i, :].unsqueeze(1).to_broadcast([P, h, ROPE // 2]),
+                    sin_sb[:, i, ROPE // 2 :].unsqueeze(1).to_broadcast([P, h, ROPE // 2]),
+                )
+                done = done + h
+                for r in range(3):
+                    if r != turning:
+                        nc.scalar.copy(out=blocks[:, r::3, :], in_=bank[:, r::3, :])
+            row = q[:].rearrange("p j c -> p (j c)")
+            nc.vector.tensor_tensor(
+                out=row.rearrange("p (b c) -> p b c", c=ROPE)[:, (2 - 8 * first) % 3 :: 3, :],
+                in0=t1[:, 0:done, :],
+                in1=t2[:, 0:done, :],
+                op=ADD,
+            )
+            nc.sync.dma_start(out=out_rows[:, i, BANK * first : BANK * (first + n)], in_=row)
 
-        idle = bank_tile()
-        keep_warm(idle, 5)
-        cast(0, 0, 1)
-        cast(0, 1, 2, nc.vector.tensor_copy)
-        cast(0, 2, 4)
-        cast(0, 4, 6, nc.vector.tensor_copy)
-        cast(0, 6, 8)
-        for g in range(XG):
-            turn(0, g, 1)
-            if g < 2:
-                keep_warm(idle, 1)
-            widen(0, g)
-            if g:
-                quant_x(0, g - 1, 1)
-        cast(1, 0, 4)
-        cast(1, 4, 8)
-        turn(1, 0, 2)
-        qa_group(0, 0)
+        idle = bank_tile(4)
+        keep_warm(idle, 4)
+        cast_sorted(0, 0)
+        cast(1, 0)
+        cast_sorted(0, 1)
+        cast(1, 1)
+        turn(6, [(0, 0)])
+        turn(5, [(1, 0)])
+        turn(7, [(0, 1), (1, 1)])
+        keep_warm(idle, 2)
+        widen(0, 0)
         widen(1, 0)
-        quant_x(0, 3, 1)
-        widen(1, 1)
+        quant_x(0, 0, 1)
+        widen(0, 1)
         quant_x(1, 0, 1)
-        turn(1, 2, 2)
-        cast(2, 0, 4)
-        widen(1, 2)
+        cast_sorted(0, 2)
+        cast(1, 2)
+        cast(1, 3)
+        widen(1, 1)
+        cast_sorted(0, 3)
+        quant_x(0, 1, 1)
+        for i in range(2):
+            qa_pass(i, 0, 0, QG * i)
+        turn(6, [(0, 2), (1, 2)])
+        for n in range(1, QG):
+            for i in range(2):
+                qa_pass(i, 0, n, QG * i + n)
+        turn(7, [(0, 3), (1, 3)])
+        widen(0, 2)
         quant_x(1, 1, 1)
-        cast(2, 4, 8)
-        qa_group(0, 1)
-        qa_group(1, 0)
+        widen(1, 2)
+        quant_x(0, 2, 1)
+        widen(0, 3)
+        quant_x(1, 2, 1)
         widen(1, 3)
-        spread(2, 0, 2)
-        quant_x(1, 2, 2)
-        spread(2, 2, 2)
+        quant_x(0, 3, 1)
+        for g in (0, 2):
+            cast(2, g)
+            cast(2, g + 1)
+            sort(2, g)
+            sort(2, g + 1)
+        qa_group(0, 1)
         qa_group(1, 1)
-        qa_group(0, 2)
-        turn(2, 0, 2)
-        turn(2, 2, 2)
+        turn(6, [(2, 0), (2, 1)])
+        turn(7, [(2, 2), (2, 3)])
         widen(2, 0)
+        quant_x(1, 3, 1)
         widen(2, 1)
-        cast(3, 0, 4)
-        cast(3, 4, 8)
-        qa_group(1, 2)
-        qa_group(0, 3)
-        spread(3, 0, 2)
+        cast_sorted(3, 0)
+        cast_sorted(3, 1)
+        cast(3, 2)
+        cast(3, 3)
+        sort(3, 2)
+        sort(3, 3)
         widen(2, 2)
-        spread(3, 2, 2)
         quant_x(2, 0, 2)
         widen(2, 3)
-        quant_x(2, 2, 2)
-        for n in range(QG):
-            round_qa(0, n)
+        qa_group(0, 2)
+        qa_group(1, 2)
+        turn(6, [(3, 0), (3, 1)])
+        qa_group(0, 3)
+        turn(7, [(3, 2), (3, 3)])
         qa_group(1, 3)
-        turn(3, 0, 2)
-        turn(3, 2, 2)
-        for n in range(QG):
-            round_qa(1, n)
+        for i in range(2):
+            for n in range(QG):
+                round_qa(i, n)
         widen(3, 0)
+        quant_x(2, 2, 2)
         widen(3, 1)
-        for g in range(XG):
-            qa_group(2, g)
         widen(3, 2)
         quant_x(3, 0, 2)
         widen(3, 3)
-        turn_qa(0)
+        for n in range(QG):
+            qa_bank(2, n, n)
         quant_x(3, 2, 2)
-        turn_qa(1)
-        quant_qa(0)
-        quant_qa(1)
-        for n in range(QG):
-            round_qa(2, n)
+        turn_qa(3, [(0, 0), (0, 1)])
+        turn_qa(4, [(0, 2), (1, 0)])
+        turn_qa(5, [(1, 1), (1, 2)])
+        round_qa(2, 0)
+        round_qa(2, 1)
+        for i in range(2):
+            for g in range(QG):
+                gather_qa(i, g)
+        for i in range(2):
+            quant_qa(i, 0, 2)
+            quant_qa(i, 2, 1)
         nc.vector.tensor_scalar(out=sin_neg[:], in0=sin_sb[:, :, 0 : ROPE // 2], scalar1=-1.0, scalar2=None, op0=MULT)
-        for n in range(QG):
-            qa_bank(3, n)
-        for n in range(QG):
+        round_qa(2, 2)
+        for n, b in enumerate((6, 7, 0)):
+            qa_bank(3, n, b)
             round_qa(3, n)
-        q_part(0, 0, 3)
-        q_part(1, 0, 3)
-        turn_qa(2)
-        quant_qa(2)
-        turn_qa(3)
-        quant_qa(3)
-        q_part(0, 3, 3)
-        q_part(1, 3, 3)
-        q_part(2, 0, 3)
-        q_part(2, 3, 3)
-        q_part(3, 0, 3)
-        q_part(3, 3, 3)
+        q_part(0, 0, (1, 2))
+        q_part(0, 2, (3,))
+        turn_qa(4, [(2, 0), (2, 1)])
+        turn_qa(5, [(2, 2), (3, 0)])
+        turn_qa(6, [(3, 1), (3, 2)])
+        for i in range(2, 4):
+            for g in range(QG):
+                gather_qa(i, g)
+        q_part(0, 3, (7,))
+        for i in range(2, 4):
+            quant_qa(i, 0, 2)
+            quant_qa(i, 2, 1)
+        q_part(0, 4, (0, 1))
+        order_kv_scales()
+        q_part(1, 0, (2, 3))
+        q_part(1, 2, (4, 5))
+        kv_fronts(6, 0)
+        q_part(1, 4, (7, 0))
+        kv_fronts(1, 2)
+        q_part(2, 0, (2, 3))
+        q_part(2, 2, (4, 5))
+        q_part(2, 4, (6, 7))
+        q_part(3, 0, (0, 1))
+        q_part(3, 2, (2, 3))
+        q_part(3, 4, (4,))
+        q_part(3, 5, (5,))
         for i in range(TILES):
-            kv_part(i, 256)
-        rope_k(0, 4)
-        for i in range(TILES):
-            kv_part(i, 0)
+            kv_back((6 + i) % 8, i)

@@ -67,7 +67,7 @@ def tile_mlaselfattn_w8_kernel(
         kscale = kept("kscale", [P, XG, 4], F32)
         cos_sb = kept("cos_sb", [P, TILES, ROPE], BF16)
         sin_sb = kept("sin_sb", [P, TILES, ROPE], BF16)
-        sin_neg = kept("sin_neg", [P, TILES, ROPE // 2], BF16)
+        factors = kept("factors", [P, TILES, 2, ROPE], BF16)
         sk_raw = kept("sk_raw", [P, KV_COLS], U8)
         xw = {(i, g): kept("xw%d_%d" % (i, g), [P, 2, P], F32) for i in range(TILES) for g in range(XG)}
         one = kept("one", [P, 8], F32)
@@ -250,11 +250,28 @@ def tile_mlaselfattn_w8_kernel(
             nc.vector.tensor_copy(out=sk[:, 0:ROPE].bitcast(I32), in_=sk_raw[:, KV_LORA:].bitcast(I32))
             nc.vector.tensor_copy(out=sk[:, ROPE:].bitcast(I32), in_=sk_raw[:, 0:KV_LORA].bitcast(I32))
 
-        def rope_terms(t1, t2, pe, c, sn, s2):
+        def make_factors():
             h = ROPE // 2
-            nc.vector.tensor_tensor(out=t2[:, :, 0:h], in0=pe[:, :, h:], in1=sn, op=MULT)
-            nc.vector.tensor_tensor(out=t2[:, :, h:], in0=pe[:, :, 0:h], in1=s2, op=MULT)
-            nc.vector.tensor_tensor(out=t1, in0=pe, in1=c, op=MULT)
+            nc.vector.tensor_copy(out=factors[:, :, 0, :], in_=cos_sb[:])
+            nc.vector.tensor_copy(out=factors[:, :, 1, 0:h], in_=sin_sb[:, :, h:])
+            nc.vector.tensor_scalar(out=factors[:, :, 1, h:], in0=sin_sb[:, :, 0:h], scalar1=-1.0, scalar2=None, op0=MULT)
+
+        def rope_terms(pe, both):
+            n = pe.shape[1]
+            terms = work.tile([P, 2, 3, ROPE], F32, name="terms", bufs=4)
+            nc.vector.tensor_tensor(
+                out=terms[:, :, 0:n, :], in0=pe.unsqueeze(1).to_broadcast([P, 2, n, ROPE]), in1=both, op=MULT
+            )
+            return terms[:, :, 0:n, :]
+
+        def rope_sum(target, terms):
+            halves = terms.rearrange("p j b (s d) -> p j b s d", s=2)
+            nc.vector.tensor_tensor(
+                out=target.rearrange("p b (s d) -> p b s d", s=2),
+                in0=halves[:, 0, :, :, :],
+                in1=halves[:, 1, :, ::-1, :],
+                op=ADD,
+            )
 
         def kv_fronts(b, first):
             bank = bank_tile(b)[:].rearrange("p (j c) -> p j c", j=2)
@@ -262,13 +279,9 @@ def tile_mlaselfattn_w8_kernel(
             for j in range(2):
                 kv_group(first + j, 0, bank[:, j, :])
             front = work.tile([P, 2, HALF], F32, name="front")
-            t1 = work.tile([P, 6, ROPE], F32, name="t1")
-            t2 = work.tile([P, 6, ROPE], F32, name="t2")
-            rope_terms(
-                t1[:, 0:2, :], t2[:, 0:2, :], bank[:, :, 0:ROPE], cos_sb[:, tiles, :], sin_neg[:, tiles, :], sin_sb[:, tiles, ROPE // 2 :]
-            )
-            nc.vector.tensor_tensor(out=front[:, :, 0:ROPE], in0=t1[:, 0:2, :], in1=t2[:, 0:2, :], op=ADD)
+            terms = rope_terms(bank[:, :, 0:ROPE], factors[:, tiles, :, :].rearrange("p i j d -> p j i d"))
             nc.scalar.copy(out=front[:, :, ROPE:], in_=bank[:, :, ROPE:])
+            rope_sum(front[:, :, 0:ROPE], terms)
             nc.sync.dma_start(out=out_rows[:, tiles, Q_COLS : Q_COLS + HALF], in_=front[:])
 
         def kv_back(b, i):
@@ -296,34 +309,22 @@ def tile_mlaselfattn_w8_kernel(
         def q_part(i, first, banks):
             n = len(banks)
             q = work.tile([P, n, BANK], F32, name="q%d" % n, bufs=6)
-            t1 = work.tile([P, 6, ROPE], F32, name="t1")
-            t2 = work.tile([P, 6, ROPE], F32, name="t2")
-            done = 0
+            sums = []
             for j, b in enumerate(banks):
                 bank = q_bank(i, first + j, b)[:].rearrange("p (b c) -> p b c", c=ROPE)
                 blocks = q[:, j, :].rearrange("p (b c) -> p b c", c=ROPE)
                 turning = (2 - 8 * (first + j)) % 3
                 h = len(range(turning, 8, 3))
-                rope_terms(
-                    t1[:, done : done + h, :],
-                    t2[:, done : done + h, :],
-                    bank[:, turning::3, :],
-                    cos_sb[:, i, :].unsqueeze(1).to_broadcast([P, h, ROPE]),
-                    sin_neg[:, i, :].unsqueeze(1).to_broadcast([P, h, ROPE // 2]),
-                    sin_sb[:, i, ROPE // 2 :].unsqueeze(1).to_broadcast([P, h, ROPE // 2]),
-                )
-                done = done + h
+                terms = rope_terms(bank[:, turning::3, :], factors[:, i, :, :].unsqueeze(2).to_broadcast([P, 2, h, ROPE]))
+                sums.append((blocks[:, turning::3, :], terms))
                 for r in range(3):
                     if r != turning:
                         nc.scalar.copy(out=blocks[:, r::3, :], in_=bank[:, r::3, :])
-            row = q[:].rearrange("p j c -> p (j c)")
-            nc.vector.tensor_tensor(
-                out=row.rearrange("p (b c) -> p b c", c=ROPE)[:, (2 - 8 * first) % 3 :: 3, :],
-                in0=t1[:, 0:done, :],
-                in1=t2[:, 0:done, :],
-                op=ADD,
+            for target, terms in sums:
+                rope_sum(target, terms)
+            nc.sync.dma_start(
+                out=out_rows[:, i, BANK * first : BANK * (first + n)], in_=q[:].rearrange("p j c -> p (j c)")
             )
-            nc.sync.dma_start(out=out_rows[:, i, BANK * first : BANK * (first + n)], in_=row)
 
         idle = bank_tile(4)
         keep_warm(idle, 4)
@@ -411,7 +412,7 @@ def tile_mlaselfattn_w8_kernel(
         for i in range(2):
             quant_qa(i, 0, 2)
             quant_qa(i, 2, 1)
-        nc.vector.tensor_scalar(out=sin_neg[:], in0=sin_sb[:, :, 0 : ROPE // 2], scalar1=-1.0, scalar2=None, op0=MULT)
+        make_factors()
         round_qa(2, 2)
         for n, b in enumerate((6, 7, 0)):
             qa_bank(3, n, b)

@@ -70,6 +70,7 @@ def tile_mlaselfattn_w8_kernel(
         factors = kept("factors", [P, TILES, 2, ROPE], BF16)
         sk_raw = kept("sk_raw", [P, KV_COLS], U8)
         xw = {(i, g): kept("xw%d_%d" % (i, g), [P, 2, P], F32) for i in range(TILES) for g in range(XG)}
+        xi = {(i, g): kept("xi%d_%d" % (i, g), [P, P, 2], F32) for i in range(2) for g in (2, 3)}
         one = kept("one", [P, 8], F32)
         ident = kept("ident", [P, P], F32)
         warm = kept("warm", [P, 8], F32)
@@ -106,18 +107,17 @@ def tile_mlaselfattn_w8_kernel(
                 )
 
         load_pair(0)
+        load_pair(1)
         nc.scalar.dma_start(out=kscale[:], in_=x_scale.rearrange("a b (g p t) -> p (a b g) t", p=P, t=4))
         nc.scalar.copy(out=warm[:, 4:8], in_=warm[:, 0:4])
         load_planes(sa, wqa_scales)
         for n in range(QG):
             load_words(wa0[n][:], wqa_words[0, :, BANK * n : BANK * (n + 1), :])
-            if n == 0:
-                load_pair(1)
         load_x(2)
         load_words(wa[1][:], wqa_words[1])
         load_words(wa[2][:], wqa_words[2])
-        load_x(3)
         load_words(wa[3][:], wqa_words[3])
+        load_x(3)
         load_planes(sb, wqb_scales)
         load_groups(wb[0][:], wqb_words[:, :, 0 : 2 * BANK, :])
         nc.sync.dma_start(out=cos_sb[:], in_=cos.rearrange("b (q i) d -> (b q) i d", i=TILES))
@@ -172,6 +172,17 @@ def tile_mlaselfattn_w8_kernel(
                 out=xg[i][:, g, :, :].rearrange("p r (u e) -> p r u e", e=2),
                 in0=turned[(i, g)].bitcast(BF16).rearrange("p u (r e) -> p r u e", e=2),
                 in1=kscale[:, g, :].rearrange("p (u e) -> p u e", e=2).unsqueeze(1).to_broadcast([P, P, 2, 2]),
+                op=MULT,
+            )
+
+        def gather_x(i, g):
+            nc.scalar.copy(out=xi[(i, g)][:], in_=turned[(i, g)].rearrange("p u r -> p r u"))
+
+        def scale_x(i, g):
+            nc.vector.tensor_tensor(
+                out=xg[i][:, g, :, :],
+                in0=xi[(i, g)][:].rearrange("p r u -> p (r u)").bitcast(BF16).rearrange("p (r t) -> p r t", t=4),
+                in1=kscale[:, g, :].unsqueeze(1).to_broadcast([P, P, 4]),
                 op=MULT,
             )
 
@@ -326,122 +337,107 @@ def tile_mlaselfattn_w8_kernel(
                 out=out_rows[:, i, BANK * first : BANK * (first + n)], in_=q[:].rearrange("p j c -> p (j c)")
             )
 
-        idle = bank_tile(4)
+        idle = bank_tile(3)
         keep_warm(idle, 4)
-        cast_sorted(0, 0)
-        cast(1, 0)
-        cast_sorted(0, 1)
-        cast(1, 1)
-        turn(6, [(0, 0)])
-        turn(5, [(1, 0)])
-        turn(7, [(0, 1), (1, 1)])
-        keep_warm(idle, 2)
+        for g in range(XG):
+            cast_sorted(0, g)
+            cast(1, g)
+        for g in range(XG):
+            turn(4 + g, [(0, g), (1, g)])
+        keep_warm(idle, 1)
+        for g in (2, 3):
+            for i in range(2):
+                gather_x(i, g)
         widen(0, 0)
         widen(1, 0)
         quant_x(0, 0, 1)
         widen(0, 1)
         quant_x(1, 0, 1)
-        cast_sorted(0, 2)
-        cast(1, 2)
-        cast(1, 3)
         widen(1, 1)
-        cast_sorted(0, 3)
         quant_x(0, 1, 1)
-        for i in range(2):
-            qa_pass(i, 0, 0, QG * i)
-        turn(6, [(0, 2), (1, 2)])
-        for n in range(1, QG):
+        for n in range(QG):
             for i in range(2):
-                qa_pass(i, 0, n, QG * i + n)
-        turn(7, [(0, 3), (1, 3)])
-        widen(0, 2)
+                qa_pass(i, 0, n, 2 * n + i)
+        scale_x(0, 2)
+        cast(2, 0)
+        cast_sorted(2, 1)
+        cast_sorted(2, 2)
+        cast(2, 3)
         quant_x(1, 1, 1)
-        widen(1, 2)
-        quant_x(0, 2, 1)
-        widen(0, 3)
-        quant_x(1, 2, 1)
-        widen(1, 3)
-        quant_x(0, 3, 1)
-        for g in (0, 2):
-            cast(2, g)
-            cast(2, g + 1)
-            sort(2, g)
-            sort(2, g + 1)
-        qa_group(0, 1)
-        qa_group(1, 1)
         turn(6, [(2, 0), (2, 1)])
         turn(7, [(2, 2), (2, 3)])
+        scale_x(1, 2)
+        quant_x(0, 2, 1)
+        scale_x(0, 3)
+        quant_x(1, 2, 1)
+        scale_x(1, 3)
+        quant_x(0, 3, 1)
         widen(2, 0)
         quant_x(1, 3, 1)
         widen(2, 1)
-        cast_sorted(3, 0)
-        cast_sorted(3, 1)
-        cast(3, 2)
-        cast(3, 3)
-        sort(3, 2)
-        sort(3, 3)
         widen(2, 2)
         quant_x(2, 0, 2)
         widen(2, 3)
-        qa_group(0, 2)
-        qa_group(1, 2)
-        turn(6, [(3, 0), (3, 1)])
-        qa_group(0, 3)
-        turn(7, [(3, 2), (3, 3)])
-        qa_group(1, 3)
+        cast_sorted(3, 0)
+        quant_x(2, 2, 2)
+        for g in range(1, XG):
+            cast_sorted(3, g)
+        for g in range(1, XG):
+            qa_group(0, g)
+            qa_group(1, g)
         for i in range(2):
             for n in range(QG):
                 round_qa(i, n)
+        qa_bank(2, 0, 6)
+        turn(0, [(3, 0), (3, 1)])
+        turn(2, [(3, 2), (3, 3)])
+        qa_bank(2, 1, 7)
+        qa_bank(2, 2, 4)
         widen(3, 0)
-        quant_x(2, 2, 2)
         widen(3, 1)
         widen(3, 2)
         quant_x(3, 0, 2)
         widen(3, 3)
-        for n in range(QG):
-            qa_bank(2, n, n)
+        make_factors()
         quant_x(3, 2, 2)
-        turn_qa(3, [(0, 0), (0, 1)])
-        turn_qa(4, [(0, 2), (1, 0)])
-        turn_qa(5, [(1, 1), (1, 2)])
         round_qa(2, 0)
         round_qa(2, 1)
+        turn_qa(1, [(0, 0), (0, 1)])
+        turn_qa(3, [(0, 2), (1, 0)])
+        turn_qa(5, [(1, 1), (1, 2)])
         for i in range(2):
             for g in range(QG):
                 gather_qa(i, g)
-        for i in range(2):
             quant_qa(i, 0, 2)
             quant_qa(i, 2, 1)
-        make_factors()
         round_qa(2, 2)
-        for n, b in enumerate((6, 7, 0)):
+        for n, b in enumerate((6, 0, 2)):
             qa_bank(3, n, b)
             round_qa(3, n)
-        q_part(0, 0, (1, 2))
-        q_part(0, 2, (3,))
-        turn_qa(4, [(2, 0), (2, 1)])
-        turn_qa(5, [(2, 2), (3, 0)])
-        turn_qa(6, [(3, 1), (3, 2)])
+        q_part(0, 0, (7, 1))
+        turn_qa(3, [(2, 0), (2, 1)])
+        turn_qa(4, [(2, 2), (3, 0)])
+        turn_qa(5, [(3, 1), (3, 2)])
         for i in range(2, 4):
             for g in range(QG):
                 gather_qa(i, g)
-        q_part(0, 3, (7,))
+        q_part(1, 0, (6, 0))
         for i in range(2, 4):
             quant_qa(i, 0, 2)
             quant_qa(i, 2, 1)
-        q_part(0, 4, (0, 1))
+        q_part(0, 2, (2, 7))
         order_kv_scales()
-        q_part(1, 0, (2, 3))
-        q_part(1, 2, (4, 5))
-        kv_fronts(6, 0)
-        q_part(1, 4, (7, 0))
-        kv_fronts(1, 2)
-        q_part(2, 0, (2, 3))
-        q_part(2, 2, (4, 5))
-        q_part(2, 4, (6, 7))
-        q_part(3, 0, (0, 1))
-        q_part(3, 2, (2, 3))
+        q_part(1, 2, (1, 3))
+        q_part(2, 0, (4, 5))
+        q_part(3, 0, (6, 0))
+        q_part(0, 4, (2, 7))
+        q_part(1, 4, (1, 3))
+        kv_fronts(4, 0)
+        q_part(2, 2, (5, 6))
+        kv_fronts(0, 2)
+        q_part(3, 2, (2, 7))
+        q_part(2, 4, (1, 3))
         q_part(3, 4, (4,))
         q_part(3, 5, (5,))
-        for i in range(TILES):
-            kv_back((6 + i) % 8, i)
+        for i, b in enumerate((6, 0, 2, 7)):
+            kv_back(b, i)

@@ -47,9 +47,8 @@ def tile_mlaselfattn_w8_kernel(
         def kept(name, shape, dtype):
             return keep.tile(shape, dtype, name=name, align_bytes=64)
 
-        xb_pair = [kept("xb_pair%d" % h, [P, 2, HIDDEN // 2], U8) for h in range(2)]
-        xb_tile = {i: kept("xb_tile%d" % i, [P, HIDDEN], U8) for i in (2, 3)}
-        xv = {(i, g): kept("xv%d_%d" % (i, g), [P, 512], BF16) for i in range(TILES) for g in range(XG)}
+        xb_early = [kept("xb_early%d" % h, [P, 2, HIDDEN // 2], U8) for h in range(2)]
+        xb_late = kept("xb_late", [P, 2, HIDDEN], U8)
         xg = [kept("xg%d" % i, [P, XG, P, 4], BF16) for i in range(TILES)]
         xc = [kept("xc%d" % i, [P, XG, P], U32) for i in range(TILES)]
         xs = [kept("xs%d" % i, [P, XG, P], U8) for i in range(TILES)]
@@ -57,8 +56,7 @@ def tile_mlaselfattn_w8_kernel(
         qg = [kept("qg%d" % i, [P, QG, P, 4], BF16) for i in range(TILES)]
         qc = [kept("qc%d" % i, [P, QG, P], U32) for i in range(TILES)]
         qs = [kept("qs%d" % i, [P, QG, P], U8) for i in range(TILES)]
-        wa0 = [kept("wa0_%d" % n, [P, BANK], U32) for n in range(QG)]
-        wa = {g: kept("wa%d" % g, [P, Q_LORA], U32) for g in range(1, XG)}
+        wa = {(g, n): kept("wa%d_%d" % (g, n), [P, BANK], U32) for g in range(XG) for n in range(QG)}
         wb = [kept("wb%d" % c, [P, QG, 2 * BANK], U32) for c in range(3)]
         wk = kept("wk", [P, XG, KV_COLS], U32)
         sa = kept("sa", [P, Q_LORA], U8)
@@ -69,8 +67,6 @@ def tile_mlaselfattn_w8_kernel(
         sin_sb = kept("sin_sb", [P, TILES, ROPE], BF16)
         factors = kept("factors", [P, TILES, 2, ROPE], BF16)
         sk_raw = kept("sk_raw", [P, KV_COLS], U8)
-        xw = {(i, g): kept("xw%d_%d" % (i, g), [P, 2, P], F32) for i in range(TILES) for g in range(XG)}
-        xi = {(i, g): kept("xi%d_%d" % (i, g), [P, P, 2], F32) for i in range(2) for g in (2, 3)}
         one = kept("one", [P, 8], F32)
         ident = kept("ident", [P, P], F32)
         warm = kept("warm", [P, 8], F32)
@@ -86,12 +82,6 @@ def tile_mlaselfattn_w8_kernel(
         nc.vector.memset(sk_raw[:].bitcast(I32), 0)
         make_identity(nc, ident[:])
 
-        def load_pair(h):
-            nc.sync.dma_start(out=xb_pair[h][:], in_=x_rows[:, 0:2, 1024 * h : 1024 * (h + 1)])
-
-        def load_x(i):
-            nc.sync.dma_start(out=xb_tile[i][:], in_=x_rows[:, i, :])
-
         def load_words(tile, words):
             nc.sync.dma_start(out=tile.bitcast(I32), in_=words.rearrange("p n t -> p (n t)").bitcast(I32))
 
@@ -106,42 +96,42 @@ def tile_mlaselfattn_w8_kernel(
                     in_=scales[:, 4 * q : 4 * q + 4, :].bitcast(I32),
                 )
 
-        load_pair(0)
-        load_pair(1)
-        nc.scalar.dma_start(out=kscale[:], in_=x_scale.rearrange("a b (g p t) -> p (a b g) t", p=P, t=4))
+        for h in range(2):
+            nc.sync.dma_start(out=xb_early[h][:], in_=x_rows[:, 0:2, 1024 * h : 1024 * (h + 1)])
+        nc.sync.dma_start(out=xb_late[:], in_=x_rows[:, 2:4, :])
+        nc.sync.dma_start(out=kscale[:], in_=x_scale.rearrange("a b (g p t) -> p (a b g) t", p=P, t=4))
         nc.scalar.copy(out=warm[:, 4:8], in_=warm[:, 0:4])
         load_planes(sa, wqa_scales)
-        for n in range(QG):
-            load_words(wa0[n][:], wqa_words[0, :, BANK * n : BANK * (n + 1), :])
-        load_x(2)
-        load_words(wa[1][:], wqa_words[1])
-        load_words(wa[2][:], wqa_words[2])
-        load_words(wa[3][:], wqa_words[3])
-        load_x(3)
-        load_planes(sb, wqb_scales)
-        load_groups(wb[0][:], wqb_words[:, :, 0 : 2 * BANK, :])
-        nc.sync.dma_start(out=cos_sb[:], in_=cos.rearrange("b (q i) d -> (b q) i d", i=TILES))
-        nc.sync.dma_start(out=sin_sb[:], in_=sin.rearrange("b (q i) d -> (b q) i d", i=TILES))
-        for c in range(1, 3):
-            load_groups(wb[c][:], wqb_words[:, :, 2 * BANK * c : 2 * BANK * (c + 1), :])
+        for g in range(XG):
+            for n in range(QG):
+                load_words(wa[(g, n)][:], wqa_words[g, :, BANK * n : BANK * (n + 1), :])
         load_planes(sk_raw, wkva_scales)
         load_groups(wk[:, :, 0:ROPE], wkva_words[:, :, KV_LORA:, :])
         load_groups(wk[:, :, ROPE:], wkva_words[:, :, 0:KV_LORA, :])
+        nc.sync.dma_start(out=cos_sb[:], in_=cos.rearrange("b (q i) d -> (b q) i d", i=TILES))
+        nc.sync.dma_start(out=sin_sb[:], in_=sin.rearrange("b (q i) d -> (b q) i d", i=TILES))
+        load_planes(sb, wqb_scales)
+        for c in range(3):
+            load_groups(wb[c][:], wqb_words[:, :, 2 * BANK * c : 2 * BANK * (c + 1), :])
 
         turned = {}
         acc = {}
 
-        sorted_units = set()
+        xv = {}
+        xw = {}
+        xi = {}
 
         def codes_of(i, g):
             if i < 2:
-                return xb_pair[g // 2][:, i, 512 * (g % 2) : 512 * (g % 2 + 1)].bitcast(FP8)
-            return xb_tile[i][:, 512 * g : 512 * (g + 1)].bitcast(FP8)
+                return xb_early[g // 2][:, i, 512 * (g % 2) : 512 * (g % 2 + 1)].bitcast(FP8)
+            return xb_late[:, i - 2, 512 * g : 512 * (g + 1)].bitcast(FP8)
 
         def cast(i, g):
+            xv[(i, g)] = kept("xv%d_%d" % (i, g), [P, 512], BF16)
             nc.scalar.copy(out=xv[(i, g)][:], in_=codes_of(i, g))
 
         def cast_sorted(i, g):
+            xw[(i, g)] = kept("xw%d_%d" % (i, g), [P, 2, P], F32)
             nc.vector.tensor_scalar(
                 out=xw[(i, g)][:].bitcast(BF16).rearrange("p u (q e) -> p q u e", e=2),
                 in0=codes_of(i, g).rearrange("p (q u e) -> p q u e", u=2, e=2),
@@ -149,17 +139,12 @@ def tile_mlaselfattn_w8_kernel(
                 scalar2=None,
                 op0=MULT,
             )
-            sorted_units.add((i, g))
-
-        def sort(i, g):
-            nc.scalar.copy(out=xw[(i, g)][:], in_=xv[(i, g)][:].bitcast(F32).rearrange("p (q u) -> p u q", u=2))
-            sorted_units.add((i, g))
 
         def turn(b, units):
             bank = bank_tile(b)[:].rearrange("p (j u r) -> p j u r", j=2, u=2)
             for j, unit in enumerate(units):
                 for u in range(2):
-                    words = xw[unit][:, u, :] if unit in sorted_units else xv[unit][:].bitcast(F32)[:, u:256:2]
+                    words = xw[unit][:, u, :] if unit in xw else xv[unit][:].bitcast(F32)[:, u:256:2]
                     nc.tensor.transpose(bank[:, j, u, :], words, ident[:])
                 turned[unit] = bank[:, j, :, :]
 
@@ -176,6 +161,7 @@ def tile_mlaselfattn_w8_kernel(
             )
 
         def gather_x(i, g):
+            xi[(i, g)] = kept("xi%d_%d" % (i, g), [P, P, 2], F32)
             nc.scalar.copy(out=xi[(i, g)][:], in_=turned[(i, g)].rearrange("p u r -> p r u"))
 
         def scale_x(i, g):
@@ -198,20 +184,20 @@ def tile_mlaselfattn_w8_kernel(
             if g == 0:
                 acc[(i, n)] = bank_tile(b)
             cols = slice(BANK * n, BANK * (n + 1))
-            words = wa[g][:, cols] if g else wa0[n][:]
             nc.tensor.matmul_mx(
                 out=acc[(i, n)][:],
                 lhsT=xc[i][:, g, :].bitcast(FP8X4),
                 lhsT_scale=xs[i][:, g, :],
-                rhs=words.bitcast(FP8X4),
+                rhs=wa[(g, n)][:].bitcast(FP8X4),
                 rhs_scale=sa[4 * g : P, cols],
                 start=(g == 0),
                 stop=(g == XG - 1),
             )
 
-        def qa_group(i, g):
+        def qa_pair(g):
             for n in range(QG):
-                qa_pass(i, g, n, QG * i + n)
+                for i in range(2):
+                    qa_pass(i, g, n, None)
 
         def qa_bank(i, n, b):
             for g in range(XG):
@@ -337,16 +323,24 @@ def tile_mlaselfattn_w8_kernel(
                 out=out_rows[:, i, BANK * first : BANK * (first + n)], in_=q[:].rearrange("p j c -> p (j c)")
             )
 
-        idle = bank_tile(3)
+        idle = bank_tile(7)
         keep_warm(idle, 4)
         for g in range(XG):
             cast_sorted(0, g)
             cast(1, g)
         for g in range(XG):
-            turn(4 + g, [(0, g), (1, g)])
-        keep_warm(idle, 1)
+            turn(g, [(0, g), (1, g)])
+            keep_warm(idle, g % 2)
+        for g in range(XG):
+            cast_sorted(2, g)
+            cast(3, g)
+        for g in range(XG):
+            turn(4 + g, [(2, g), (3, g)])
         for g in (2, 3):
             for i in range(2):
+                gather_x(i, g)
+        for g in (0, 1):
+            for i in (2, 3):
                 gather_x(i, g)
         widen(0, 0)
         widen(1, 0)
@@ -355,89 +349,70 @@ def tile_mlaselfattn_w8_kernel(
         quant_x(1, 0, 1)
         widen(1, 1)
         quant_x(0, 1, 1)
-        for n in range(QG):
-            for i in range(2):
-                qa_pass(i, 0, n, 2 * n + i)
         scale_x(0, 2)
-        cast(2, 0)
-        cast_sorted(2, 1)
-        cast_sorted(2, 2)
-        cast(2, 3)
         quant_x(1, 1, 1)
-        turn(6, [(2, 0), (2, 1)])
-        turn(7, [(2, 2), (2, 3)])
         scale_x(1, 2)
         quant_x(0, 2, 1)
         scale_x(0, 3)
         quant_x(1, 2, 1)
         scale_x(1, 3)
         quant_x(0, 3, 1)
-        widen(2, 0)
+        scale_x(2, 0)
         quant_x(1, 3, 1)
-        widen(2, 1)
+        scale_x(2, 1)
         widen(2, 2)
         quant_x(2, 0, 2)
         widen(2, 3)
-        cast_sorted(3, 0)
-        quant_x(2, 2, 2)
-        for g in range(1, XG):
-            cast_sorted(3, g)
-        for g in range(1, XG):
-            qa_group(0, g)
-            qa_group(1, g)
-        for i in range(2):
-            for n in range(QG):
-                round_qa(i, n)
-        qa_bank(2, 0, 6)
-        turn(0, [(3, 0), (3, 1)])
-        turn(2, [(3, 2), (3, 3)])
-        qa_bank(2, 1, 7)
-        qa_bank(2, 2, 4)
-        widen(3, 0)
-        widen(3, 1)
         widen(3, 2)
-        quant_x(3, 0, 2)
+        quant_x(2, 2, 2)
         widen(3, 3)
-        make_factors()
+        scale_x(3, 0)
         quant_x(3, 2, 2)
-        round_qa(2, 0)
-        round_qa(2, 1)
-        turn_qa(1, [(0, 0), (0, 1)])
-        turn_qa(3, [(0, 2), (1, 0)])
-        turn_qa(5, [(1, 1), (1, 2)])
-        for i in range(2):
-            for g in range(QG):
-                gather_qa(i, g)
-            quant_qa(i, 0, 2)
-            quant_qa(i, 2, 1)
-        round_qa(2, 2)
-        for n, b in enumerate((6, 0, 2)):
+        scale_x(3, 1)
+        order_kv_scales()
+        quant_x(3, 0, 2)
+        make_factors()
+        for n, banks in enumerate(((0, 2), (1, 3), (4, 5))):
+            for i in range(2):
+                qa_pass(i, 0, n, banks[i])
+        for g in range(1, XG):
+            qa_pair(g)
+        for n in range(QG):
+            for i in range(2):
+                round_qa(i, n)
+        for n, b in enumerate((0, 2, 1)):
+            qa_bank(2, n, b)
+            round_qa(2, n)
+        for n, b in enumerate((6, 7, 3)):
             qa_bank(3, n, b)
             round_qa(3, n)
-        q_part(0, 0, (7, 1))
-        turn_qa(3, [(2, 0), (2, 1)])
-        turn_qa(4, [(2, 2), (3, 0)])
-        turn_qa(5, [(3, 1), (3, 2)])
+        kv_fronts(4, 0)
+        units = [(i, g) for i in range(TILES) for g in range(QG)]
+        for j, b in enumerate((5, 0, 2, 1, 6, 7)):
+            turn_qa(b, units[2 * j : 2 * j + 2])
+        for i in range(2):
+            for g in range(QG):
+                gather_qa(i, g)
+            quant_qa(i, 0, 2)
+            quant_qa(i, 2, 1)
+        kv_fronts(3, 2)
         for i in range(2, 4):
             for g in range(QG):
                 gather_qa(i, g)
-        q_part(1, 0, (6, 0))
+        q_part(0, 0, (4, 5))
         for i in range(2, 4):
             quant_qa(i, 0, 2)
             quant_qa(i, 2, 1)
-        q_part(0, 2, (2, 7))
-        order_kv_scales()
-        q_part(1, 2, (1, 3))
-        q_part(2, 0, (4, 5))
-        q_part(3, 0, (6, 0))
-        q_part(0, 4, (2, 7))
-        q_part(1, 4, (1, 3))
-        kv_fronts(4, 0)
-        q_part(2, 2, (5, 6))
-        kv_fronts(0, 2)
-        q_part(3, 2, (2, 7))
-        q_part(2, 4, (1, 3))
-        q_part(3, 4, (4,))
-        q_part(3, 5, (5,))
-        for i, b in enumerate((6, 0, 2, 7)):
+        q_part(1, 0, (0, 2))
+        q_part(2, 0, (3, 1))
+        q_part(3, 0, (6, 7))
+        for n in (2, 4):
+            q_part(0, n, (4, 5))
+            q_part(1, n, (0, 2))
+            q_part(2, n, (3, 1))
+            if n == 2:
+                q_part(3, n, (6, 7))
+        q_part(3, 4, (6,))
+        q_part(3, 5, (7,))
+        for i, b in enumerate((4, 5, 0, 2)):
             kv_back(b, i)

@@ -20,6 +20,7 @@ FP8 = mybir.dt.float8_e4m3fn
 FP8X4 = mybir.dt.float8_e4m3fn_x4
 MULT = mybir.AluOpType.mult
 ADD = mybir.AluOpType.add
+COPY = mybir.ActivationFunctionType.Copy
 
 P = 128
 BANK = 512
@@ -72,6 +73,9 @@ def tile_mlaselfattn_w8_kernel(
         warm = kept("warm", [P, 8], F32)
         zeros = kept("zeros", [P, BANK], BF16)
 
+        piece_order = [(g, n) for g in range(2) for n in range(2)] + [(g, 2) for g in range(2)]
+        piece_order = piece_order + [(g, n) for g in range(2, XG) for n in range(QG)]
+
         ctx.enter_context(tc.manual_schedule())
 
         nc.vector.memset(sa[:].bitcast(I32), 0)
@@ -98,13 +102,12 @@ def tile_mlaselfattn_w8_kernel(
 
         for h in range(2):
             nc.sync.dma_start(out=xb_early[h][:], in_=x_rows[:, 0:2, 1024 * h : 1024 * (h + 1)])
-        nc.sync.dma_start(out=xb_late[:], in_=x_rows[:, 2:4, :])
         nc.sync.dma_start(out=kscale[:], in_=x_scale.rearrange("a b (g p t) -> p (a b g) t", p=P, t=4))
+        nc.sync.dma_start(out=xb_late[:], in_=x_rows[:, 2:4, :])
         nc.scalar.copy(out=warm[:, 4:8], in_=warm[:, 0:4])
         load_planes(sa, wqa_scales)
-        for g in range(XG):
-            for n in range(QG):
-                load_words(wa[(g, n)][:], wqa_words[g, :, BANK * n : BANK * (n + 1), :])
+        for g, n in piece_order:
+            load_words(wa[(g, n)][:], wqa_words[g, :, BANK * n : BANK * (n + 1), :])
         load_planes(sk_raw, wkva_scales)
         load_groups(wk[:, :, 0:ROPE], wkva_words[:, :, KV_LORA:, :])
         load_groups(wk[:, :, ROPE:], wkva_words[:, :, 0:KV_LORA, :])
@@ -120,6 +123,7 @@ def tile_mlaselfattn_w8_kernel(
         xv = {}
         xw = {}
         xi = {}
+        planes = {}
 
         def codes_of(i, g):
             if i < 2:
@@ -146,7 +150,7 @@ def tile_mlaselfattn_w8_kernel(
                 for u in range(2):
                     words = xw[unit][:, u, :] if unit in xw else xv[unit][:].bitcast(F32)[:, u:256:2]
                     nc.tensor.transpose(bank[:, j, u, :], words, ident[:])
-                turned[unit] = bank[:, j, :, :]
+            turned[units[0]] = bank
 
         def keep_warm(bank, n):
             for j in range(n):
@@ -155,19 +159,34 @@ def tile_mlaselfattn_w8_kernel(
         def widen(i, g):
             nc.vector.tensor_tensor(
                 out=xg[i][:, g, :, :].rearrange("p r (u e) -> p r u e", e=2),
-                in0=turned[(i, g)].bitcast(BF16).rearrange("p u (r e) -> p r u e", e=2),
+                in0=turned[(i - i % 2, g)][:, i % 2, :, :].bitcast(BF16).rearrange("p u (r e) -> p r u e", e=2),
                 in1=kscale[:, g, :].rearrange("p (u e) -> p u e", e=2).unsqueeze(1).to_broadcast([P, P, 2, 2]),
                 op=MULT,
             )
 
-        def gather_x(i, g):
-            xi[(i, g)] = kept("xi%d_%d" % (i, g), [P, P, 2], F32)
-            nc.scalar.copy(out=xi[(i, g)][:], in_=turned[(i, g)].rearrange("p u r -> p r u"))
+        def scale_planes(g):
+            planes[g] = kept("planes%d" % g, [P, 2, 4, P], BF16)
+            values = turned[(2, g)].bitcast(BF16).rearrange("p j u (r e) -> p j u r e", e=2)
+            for t in range(4):
+                nc.scalar.activation(
+                    out=planes[g][:, :, t, :], in_=values[:, :, t // 2, :, t % 2], func=COPY, scale=kscale[:, g, t : t + 1]
+                )
+
+        def weave(i, g):
+            nc.vector.tensor_copy(out=xg[i][:, g, :, :], in_=planes[g][:, i - 2, :, :].rearrange("p t r -> p r t"))
+
+        def gather_x(first, g):
+            xi[(first, g)] = kept("xi%d_%d" % (first, g), [P, 2, P, 2], F32)
+            nc.scalar.copy(out=xi[(first, g)][:], in_=turned[(first, g)].rearrange("p j u r -> p j r u"))
+
+        def gathered(i, g):
+            words = xi[(i - i % 2, g)][:, i % 2, :, :]
+            return words.rearrange("p r u -> p (r u)").bitcast(BF16).rearrange("p (r t) -> p r t", t=4)
 
         def scale_x(i, g):
             nc.vector.tensor_tensor(
                 out=xg[i][:, g, :, :],
-                in0=xi[(i, g)][:].rearrange("p r u -> p (r u)").bitcast(BF16).rearrange("p (r t) -> p r t", t=4),
+                in0=gathered(i, g),
                 in1=kscale[:, g, :].unsqueeze(1).to_broadcast([P, P, 4]),
                 op=MULT,
             )
@@ -181,7 +200,7 @@ def tile_mlaselfattn_w8_kernel(
             )
 
         def qa_pass(i, g, n, b):
-            if g == 0:
+            if (i, n) not in acc:
                 acc[(i, n)] = bank_tile(b)
             cols = slice(BANK * n, BANK * (n + 1))
             nc.tensor.matmul_mx(
@@ -209,26 +228,23 @@ def tile_mlaselfattn_w8_kernel(
                 in_=acc[(i, n)][:].rearrange("p (q u e) -> p u q e", u=2, e=2),
             )
 
-        def turn_qa(b, units):
-            bank = bank_tile(b)[:].rearrange("p (j u r) -> p j u r", j=2, u=2)
-            for j, (i, g) in enumerate(units):
-                words = qv[i][:, g, :].bitcast(F32)
-                for u in range(2):
-                    nc.tensor.transpose(bank[:, j, u, :], words[:, P * u : P * (u + 1)], ident[:])
-                turned[("qa", i, g)] = bank[:, j, :, :]
+        def turn_qa(i, g, half):
+            words = qv[i][:, g, :].bitcast(F32)
+            for u in range(2):
+                nc.tensor.transpose(half[:, P * u : P * (u + 1)], words[:, P * u : P * (u + 1)], ident[:])
+            turned[("qa", i, g)] = half
 
         def gather_qa(i, g):
             nc.scalar.copy(
                 out=qg[i][:, g, :, :].rearrange("p r t -> p (r t)").bitcast(F32).rearrange("p (r u) -> p r u", u=2),
-                in_=turned[("qa", i, g)].rearrange("p u r -> p r u"),
+                in_=turned[("qa", i, g)].rearrange("p (u r) -> p r u", u=2),
             )
 
-        def quant_qa(i, g, n):
-            gs = slice(g, g + n)
+        def quant_qa(i):
             nc.vector.quantize_mx(
-                out=qc[i][:, gs, :].rearrange("p g r -> p (g r)").bitcast(FP8X4),
-                scales=qs[i][:, gs, :].rearrange("p g r -> p (g r)"),
-                in_=qg[i][:, gs, :, :].rearrange("p g r t -> p (g r t)"),
+                out=qc[i][:].rearrange("p g r -> p (g r)").bitcast(FP8X4),
+                scales=qs[i][:].rearrange("p g r -> p (g r)"),
+                in_=qg[i][:].rearrange("p g r t -> p (g r t)"),
             )
 
         def kv_group(i, first, target):
@@ -325,26 +341,38 @@ def tile_mlaselfattn_w8_kernel(
 
         idle = bank_tile(7)
         keep_warm(idle, 4)
-        for g in range(XG):
+        cast_sorted(0, 0)
+        cast_sorted(1, 0)
+        for g in range(1, XG):
             cast_sorted(0, g)
             cast(1, g)
-        for g in range(XG):
-            turn(g, [(0, g), (1, g)])
-            keep_warm(idle, g % 2)
-        for g in range(XG):
-            cast_sorted(2, g)
-            cast(3, g)
-        for g in range(XG):
-            turn(4 + g, [(2, g), (3, g)])
-        for g in (2, 3):
-            for i in range(2):
-                gather_x(i, g)
-        for g in (0, 1):
-            for i in (2, 3):
-                gather_x(i, g)
+        turn(0, [(0, 0), (1, 0)])
+        turn(1, [(0, 1), (1, 1)])
+        keep_warm(idle, 1)
+        turn(2, [(0, 2), (1, 2)])
+        turn(3, [(0, 3), (1, 3)])
         widen(0, 0)
-        widen(1, 0)
+        cast_sorted(2, 0)
+        cast(3, 0)
+        cast_sorted(2, 1)
+        cast(3, 1)
+        cast_sorted(2, 2)
+        cast(3, 2)
+        cast_sorted(2, 3)
+        cast(3, 3)
+        turn(4, [(2, 0), (3, 0)])
+        keep_warm(idle, 1)
+        turn(5, [(2, 1), (3, 1)])
+        turn(6, [(2, 2), (3, 2)])
+        turn(7, [(2, 3), (3, 3)])
+        gather_x(0, 2)
+        gather_x(0, 3)
+        gather_x(2, 0)
+        gather_x(2, 1)
+        scale_planes(2)
+        scale_planes(3)
         quant_x(0, 0, 1)
+        widen(1, 0)
         widen(0, 1)
         quant_x(1, 0, 1)
         widen(1, 1)
@@ -360,59 +388,51 @@ def tile_mlaselfattn_w8_kernel(
         scale_x(2, 0)
         quant_x(1, 3, 1)
         scale_x(2, 1)
-        widen(2, 2)
+        weave(2, 2)
         quant_x(2, 0, 2)
-        widen(2, 3)
-        widen(3, 2)
+        weave(2, 3)
+        weave(3, 2)
         quant_x(2, 2, 2)
-        widen(3, 3)
+        weave(3, 3)
         scale_x(3, 0)
         quant_x(3, 2, 2)
         scale_x(3, 1)
         order_kv_scales()
         quant_x(3, 0, 2)
         make_factors()
-        for n, banks in enumerate(((0, 2), (1, 3), (4, 5))):
+        banks = ((0, 2), (3, 1), (4, 5))
+        for g, n in piece_order:
             for i in range(2):
-                qa_pass(i, 0, n, banks[i])
-        for g in range(1, XG):
-            qa_pair(g)
+                qa_pass(i, g, n, banks[n][i])
         for n in range(QG):
             for i in range(2):
                 round_qa(i, n)
-        for n, b in enumerate((0, 2, 1)):
+        for n, b in enumerate((0, 2, 3)):
             qa_bank(2, n, b)
             round_qa(2, n)
-        for n, b in enumerate((6, 7, 3)):
+        for n, b in enumerate((6, 7, 1)):
             qa_bank(3, n, b)
             round_qa(3, n)
         kv_fronts(4, 0)
         units = [(i, g) for i in range(TILES) for g in range(QG)]
-        for j, b in enumerate((5, 0, 2, 1, 6, 7)):
-            turn_qa(b, units[2 * j : 2 * j + 2])
-        for i in range(2):
+        for j, b in enumerate((5, 0, 2, 3, 6, 7)):
+            bank = bank_tile(b)
+            for k in range(2):
+                i, g = units[2 * j + k]
+                turn_qa(i, g, bank[:, HALF * k : HALF * (k + 1)])
+        for i in range(TILES):
             for g in range(QG):
                 gather_qa(i, g)
-            quant_qa(i, 0, 2)
-            quant_qa(i, 2, 1)
-        kv_fronts(3, 2)
-        for i in range(2, 4):
-            for g in range(QG):
-                gather_qa(i, g)
-        q_part(0, 0, (4, 5))
-        for i in range(2, 4):
-            quant_qa(i, 0, 2)
-            quant_qa(i, 2, 1)
-        q_part(1, 0, (0, 2))
-        q_part(2, 0, (3, 1))
-        q_part(3, 0, (6, 7))
-        for n in (2, 4):
-            q_part(0, n, (4, 5))
-            q_part(1, n, (0, 2))
-            q_part(2, n, (3, 1))
-            if n == 2:
-                q_part(3, n, (6, 7))
-        q_part(3, 4, (6,))
-        q_part(3, 5, (7,))
+            if i:
+                quant_qa(i - 1)
+        quant_qa(TILES - 1)
+        kv_fronts(1, 2)
+        pairs = ((4, 5), (0, 2), (3, 6), (7, 1))
+        for n in range(0, 6, 2):
+            for i in range(TILES):
+                if (i, n) != (3, 4):
+                    q_part(i, n, pairs[i])
+        q_part(3, 4, (7,))
+        q_part(3, 5, (1,))
         for i, b in enumerate((4, 5, 0, 2)):
             kv_back(b, i)

@@ -57,7 +57,6 @@ def tile_mlaselfattn_w8_kernel(
         qg = [kept("qg%d" % i, [P, QG, P, 4], BF16) for i in range(TILES)]
         qc = [kept("qc%d" % i, [P, QG, P], U32) for i in range(TILES)]
         qs = [kept("qs%d" % i, [P, QG, P], U8) for i in range(TILES)]
-        wa = {(g, n): kept("wa%d_%d" % (g, n), [P, BANK], U32) for g in range(XG) for n in range(QG)}
         wb = [kept("wb%d" % c, [P, QG, 2 * BANK], U32) for c in range(3)]
         wk = kept("wk", [P, XG, KV_COLS], U32)
         sa = kept("sa", [P, Q_LORA], U8)
@@ -73,8 +72,14 @@ def tile_mlaselfattn_w8_kernel(
         warm = kept("warm", [P, 8], F32)
         zeros = kept("zeros", [P, BANK], BF16)
 
-        piece_order = [(g, n) for g in range(2) for n in range(2)] + [(g, 2) for g in range(2)]
-        piece_order = piece_order + [(g, n) for g in range(2, XG) for n in range(QG)]
+        pieces = [(0, 0, 2), (1, 0, 2), (0, 2, 1), (1, 2, 1), (2, 0, 2), (2, 2, 1)] + [(3, n, 1) for n in range(QG)]
+        wa = {}
+        for g, first, count in pieces:
+            piece = kept("wa%d_%d" % (g, first), [P, count * BANK], U32)
+            wa[("piece", g, first)] = piece
+            for n in range(count):
+                wa[(g, first + n)] = piece[:, BANK * n : BANK * (n + 1)]
+        piece_order = [(g, first + n) for g, first, count in pieces for n in range(count)]
 
         ctx.enter_context(tc.manual_schedule())
 
@@ -82,7 +87,7 @@ def tile_mlaselfattn_w8_kernel(
         nc.vector.memset(zeros[:].bitcast(I32), 0)
         nc.vector.memset(warm[:], 0.0)
         nc.vector.memset(one[:], 1.0)
-        nc.vector.memset(sb[:].bitcast(I32), 0)
+        nc.vector.memset(sb[:, 64:].bitcast(I32), 0)
         nc.vector.memset(sk_raw[:].bitcast(I32), 0)
         make_identity(nc, ident[:])
 
@@ -92,10 +97,10 @@ def tile_mlaselfattn_w8_kernel(
         def load_groups(tile, words):
             nc.sync.dma_start(out=tile.bitcast(I32), in_=words.rearrange("g p n t -> p g (n t)").bitcast(I32))
 
-        def load_planes(tile, scales):
+        def load_planes(tile, scales, queue):
             groups = scales.shape[0]
             for q in range(4):
-                nc.sync.dma_start(
+                queue.dma_start(
                     out=tile[32 * q : 32 * q + 4 * groups, :].bitcast(I32),
                     in_=scales[:, 4 * q : 4 * q + 4, :].bitcast(I32),
                 )
@@ -105,17 +110,17 @@ def tile_mlaselfattn_w8_kernel(
         nc.sync.dma_start(out=kscale[:], in_=x_scale.rearrange("a b (g p t) -> p (a b g) t", p=P, t=4))
         nc.sync.dma_start(out=xb_late[:], in_=x_rows[:, 2:4, :])
         nc.scalar.copy(out=warm[:, 4:8], in_=warm[:, 0:4])
-        load_planes(sa, wqa_scales)
-        for g, n in piece_order:
-            load_words(wa[(g, n)][:], wqa_words[g, :, BANK * n : BANK * (n + 1), :])
-        load_planes(sk_raw, wkva_scales)
+        load_planes(sa, wqa_scales, nc.sync)
+        for g, first, count in pieces:
+            load_words(wa[("piece", g, first)][:], wqa_words[g, :, BANK * first : BANK * (first + count), :])
+        load_planes(sk_raw, wkva_scales, nc.sync)
         load_groups(wk[:, :, 0:ROPE], wkva_words[:, :, KV_LORA:, :])
-        load_groups(wk[:, :, ROPE:], wkva_words[:, :, 0:KV_LORA, :])
+        load_groups(wk[:, :, ROPE:HALF], wkva_words[:, :, 0 : HALF - ROPE, :])
         nc.sync.dma_start(out=cos_sb[:], in_=cos.rearrange("b (q i) d -> (b q) i d", i=TILES))
         nc.sync.dma_start(out=sin_sb[:], in_=sin.rearrange("b (q i) d -> (b q) i d", i=TILES))
-        load_planes(sb, wqb_scales)
         for c in range(3):
             load_groups(wb[c][:], wqb_words[:, :, 2 * BANK * c : 2 * BANK * (c + 1), :])
+        load_groups(wk[:, :, HALF:], wkva_words[:, :, HALF - ROPE : KV_LORA, :])
 
         turned = {}
         acc = {}
@@ -207,7 +212,7 @@ def tile_mlaselfattn_w8_kernel(
                 out=acc[(i, n)][:],
                 lhsT=xc[i][:, g, :].bitcast(FP8X4),
                 lhsT_scale=xs[i][:, g, :],
-                rhs=wa[(g, n)][:].bitcast(FP8X4),
+                rhs=wa[(g, n)].bitcast(FP8X4),
                 rhs_scale=sa[4 * g : P, cols],
                 start=(g == 0),
                 stop=(g == XG - 1),
@@ -385,6 +390,8 @@ def tile_mlaselfattn_w8_kernel(
         quant_x(1, 2, 1)
         scale_x(1, 3)
         quant_x(0, 3, 1)
+        nc.vector.memset(sb[:, 0:64].bitcast(I32), 0)
+        load_planes(sb, wqb_scales, nc.gpsimd)
         scale_x(2, 0)
         quant_x(1, 3, 1)
         scale_x(2, 1)
@@ -397,9 +404,9 @@ def tile_mlaselfattn_w8_kernel(
         scale_x(3, 0)
         quant_x(3, 2, 2)
         scale_x(3, 1)
-        order_kv_scales()
-        quant_x(3, 0, 2)
         make_factors()
+        quant_x(3, 0, 2)
+        order_kv_scales()
         banks = ((0, 2), (3, 1), (4, 5))
         for g, n in piece_order:
             for i in range(2):

@@ -79,7 +79,6 @@ def tile_mlaselfattn_w8_kernel(
             wa[("piece", g, first)] = piece
             for n in range(count):
                 wa[(g, first + n)] = piece[:, BANK * n : BANK * (n + 1)]
-        piece_order = [(g, first + n) for g, first, count in pieces for n in range(count)]
 
         ctx.enter_context(tc.manual_schedule())
 
@@ -218,15 +217,6 @@ def tile_mlaselfattn_w8_kernel(
                 stop=(g == XG - 1),
             )
 
-        def qa_pair(g):
-            for n in range(QG):
-                for i in range(2):
-                    qa_pass(i, g, n, None)
-
-        def qa_bank(i, n, b):
-            for g in range(XG):
-                qa_pass(i, g, n, b)
-
         def round_qa(i, n):
             nc.scalar.copy(
                 out=qv[i][:, n, :].rearrange("p (u q e) -> p u q e", u=2, e=2),
@@ -309,27 +299,28 @@ def tile_mlaselfattn_w8_kernel(
             nc.scalar.copy(out=back[:], in_=bank[:, 0:HALF])
             nc.sync.dma_start(out=out_rows[:, i, Q_COLS + HALF :], in_=back[:])
 
-        def q_bank(i, n, b):
-            bank = bank_tile(b)
-            cols = slice(BANK * n, BANK * (n + 1))
+        def q_banks(i, first, banks):
+            tiles = [bank_tile(b) for b in banks]
             for g in range(QG):
-                nc.tensor.matmul_mx(
-                    out=bank[:],
-                    lhsT=qc[i][:, g, :].bitcast(FP8X4),
-                    lhsT_scale=qs[i][:, g, :],
-                    rhs=wb[n // 2][:, g, BANK * (n % 2) : BANK * (n % 2 + 1)].bitcast(FP8X4),
-                    rhs_scale=sb[4 * g : P, cols],
-                    start=(g == 0),
-                    stop=(g == QG - 1),
-                )
-            return bank
+                for j, bank in enumerate(tiles):
+                    n = first + j
+                    nc.tensor.matmul_mx(
+                        out=bank[:],
+                        lhsT=qc[i][:, g, :].bitcast(FP8X4),
+                        lhsT_scale=qs[i][:, g, :],
+                        rhs=wb[n // 2][:, g, BANK * (n % 2) : BANK * (n % 2 + 1)].bitcast(FP8X4),
+                        rhs_scale=sb[4 * g : P, BANK * n : BANK * (n + 1)],
+                        start=(g == 0),
+                        stop=(g == QG - 1),
+                    )
+            return tiles
 
         def q_part(i, first, banks):
             n = len(banks)
             q = work.tile([P, n, BANK], F32, name="q%d" % n, bufs=6)
             sums = []
-            for j, b in enumerate(banks):
-                bank = q_bank(i, first + j, b)[:].rearrange("p (b c) -> p b c", c=ROPE)
+            for j, whole in enumerate(q_banks(i, first, banks)):
+                bank = whole[:].rearrange("p (b c) -> p b c", c=ROPE)
                 blocks = q[:, j, :].rearrange("p (b c) -> p b c", c=ROPE)
                 turning = (2 - 8 * (first + j)) % 3
                 h = len(range(turning, 8, 3))
@@ -408,21 +399,22 @@ def tile_mlaselfattn_w8_kernel(
         quant_x(3, 0, 2)
         order_kv_scales()
         banks = ((0, 2), (3, 1), (4, 5))
-        for g, n in piece_order:
+        for g, first, count in pieces:
             for i in range(2):
-                qa_pass(i, g, n, banks[n][i])
+                for n in range(first, first + count):
+                    qa_pass(i, g, n, banks[n][i])
         for n in range(QG):
             for i in range(2):
                 round_qa(i, n)
-        for n, b in enumerate((0, 2, 3)):
-            qa_bank(2, n, b)
-            round_qa(2, n)
-        for n, b in enumerate((6, 7, 1)):
-            qa_bank(3, n, b)
-            round_qa(3, n)
+        for i, three in ((2, (6, 7, 0)), (3, (2, 3, 1))):
+            for g in range(XG):
+                for n in range(QG):
+                    qa_pass(i, g, n, three[n])
+            for n in range(QG):
+                round_qa(i, n)
         kv_fronts(4, 0)
         units = [(i, g) for i in range(TILES) for g in range(QG)]
-        for j, b in enumerate((5, 0, 2, 3, 6, 7)):
+        for j, b in enumerate((5, 6, 7, 0, 2, 3)):
             bank = bank_tile(b)
             for k in range(2):
                 i, g = units[2 * j + k]
@@ -434,12 +426,12 @@ def tile_mlaselfattn_w8_kernel(
                 quant_qa(i - 1)
         quant_qa(TILES - 1)
         kv_fronts(1, 2)
-        pairs = ((4, 5), (0, 2), (3, 6), (7, 1))
+        pairs = ((4, 5), (6, 7), (0, 2), (3, 1))
         for n in range(0, 6, 2):
             for i in range(TILES):
                 if (i, n) != (3, 4):
                     q_part(i, n, pairs[i])
-        q_part(3, 4, (7,))
+        q_part(3, 4, (3,))
         q_part(3, 5, (1,))
-        for i, b in enumerate((4, 5, 0, 2)):
+        for i, b in enumerate((4, 5, 6, 7)):
             kv_back(b, i)

@@ -20,7 +20,6 @@ FP8 = mybir.dt.float8_e4m3fn
 FP8X4 = mybir.dt.float8_e4m3fn_x4
 MULT = mybir.AluOpType.mult
 ADD = mybir.AluOpType.add
-COPY = mybir.ActivationFunctionType.Copy
 
 P = 128
 BANK = 512
@@ -49,7 +48,7 @@ def tile_mlaselfattn_w8_kernel(
             return keep.tile(shape, dtype, name=name, align_bytes=64)
 
         xb_early = [kept("xb_early%d" % h, [P, 2, HIDDEN // 2], U8) for h in range(2)]
-        xb_late = kept("xb_late", [P, 2, HIDDEN], U8)
+        xb_late = [kept("xb_late%d" % j, [P, HIDDEN], U8) for j in range(2)]
         xg = [kept("xg%d" % i, [P, XG, P, 4], BF16) for i in range(TILES)]
         xc = [kept("xc%d" % i, [P, XG, P], U32) for i in range(TILES)]
         xs = [kept("xs%d" % i, [P, XG, P], U8) for i in range(TILES)]
@@ -57,22 +56,21 @@ def tile_mlaselfattn_w8_kernel(
         qg = [kept("qg%d" % i, [P, QG, P, 4], BF16) for i in range(TILES)]
         qc = [kept("qc%d" % i, [P, QG, P], U32) for i in range(TILES)]
         qs = [kept("qs%d" % i, [P, QG, P], U8) for i in range(TILES)]
-        wb = [kept("wb%d" % c, [P, QG, 2 * BANK], U32) for c in range(3)]
-        wk = kept("wk", [P, XG, KV_COLS], U32)
+        wb = [kept("wb%d" % c, [P, QG, 3 * BANK], U32) for c in range(2)]
+        wk = kept("wk", [P, XG, ROPE + KV_COLS], U32)
         sa = kept("sa", [P, Q_LORA], U8)
         sb = kept("sb", [P, Q_COLS], U8)
-        sk = kept("sk", [P, KV_COLS], U8)
+        sk = kept("sk", [P, ROPE + KV_COLS], U8)
         kscale = kept("kscale", [P, XG, 4], F32)
         cos_sb = kept("cos_sb", [P, TILES, ROPE], BF16)
         sin_sb = kept("sin_sb", [P, TILES, ROPE], BF16)
         factors = kept("factors", [P, TILES, 2, ROPE], BF16)
-        sk_raw = kept("sk_raw", [P, KV_COLS], U8)
         one = kept("one", [P, 8], F32)
         ident = kept("ident", [P, P], F32)
         warm = kept("warm", [P, 8], F32)
         zeros = kept("zeros", [P, BANK], BF16)
 
-        pieces = [(0, 0, 2), (1, 0, 2), (0, 2, 1), (1, 2, 1), (2, 0, 2), (2, 2, 1)] + [(3, n, 1) for n in range(QG)]
+        pieces = [(0, 0, 2), (1, 0, 2), (0, 2, 1), (1, 2, 1), (2, 0, 3), (3, 0, 2), (3, 2, 1)]
         wa = {}
         for g, first, count in pieces:
             piece = kept("wa%d_%d" % (g, first), [P, count * BANK], U32)
@@ -87,7 +85,7 @@ def tile_mlaselfattn_w8_kernel(
         nc.vector.memset(warm[:], 0.0)
         nc.vector.memset(one[:], 1.0)
         nc.vector.memset(sb[:, 64:].bitcast(I32), 0)
-        nc.vector.memset(sk_raw[:].bitcast(I32), 0)
+        nc.vector.memset(sk[:, ROPE:].bitcast(I32), 0)
         make_identity(nc, ident[:])
 
         def load_words(tile, words):
@@ -100,26 +98,25 @@ def tile_mlaselfattn_w8_kernel(
             groups = scales.shape[0]
             for q in range(4):
                 queue.dma_start(
-                    out=tile[32 * q : 32 * q + 4 * groups, :].bitcast(I32),
+                    out=tile[32 * q : 32 * q + 4 * groups].bitcast(I32),
                     in_=scales[:, 4 * q : 4 * q + 4, :].bitcast(I32),
                 )
 
         for h in range(2):
             nc.sync.dma_start(out=xb_early[h][:], in_=x_rows[:, 0:2, 1024 * h : 1024 * (h + 1)])
         nc.sync.dma_start(out=kscale[:], in_=x_scale.rearrange("a b (g p t) -> p (a b g) t", p=P, t=4))
-        nc.sync.dma_start(out=xb_late[:], in_=x_rows[:, 2:4, :])
+        for j in range(2):
+            nc.sync.dma_start(out=xb_late[j][:], in_=x_rows[:, 2 + j, :])
         nc.scalar.copy(out=warm[:, 4:8], in_=warm[:, 0:4])
-        load_planes(sa, wqa_scales, nc.sync)
+        load_planes(sa[:], wqa_scales, nc.sync)
         for g, first, count in pieces:
             load_words(wa[("piece", g, first)][:], wqa_words[g, :, BANK * first : BANK * (first + count), :])
-        load_planes(sk_raw, wkva_scales, nc.sync)
-        load_groups(wk[:, :, 0:ROPE], wkva_words[:, :, KV_LORA:, :])
-        load_groups(wk[:, :, ROPE:HALF], wkva_words[:, :, 0 : HALF - ROPE, :])
+        load_planes(sk[:, ROPE:], wkva_scales, nc.sync)
+        load_groups(wk[:, :, ROPE:], wkva_words)
         nc.sync.dma_start(out=cos_sb[:], in_=cos.rearrange("b (q i) d -> (b q) i d", i=TILES))
         nc.sync.dma_start(out=sin_sb[:], in_=sin.rearrange("b (q i) d -> (b q) i d", i=TILES))
-        for c in range(3):
-            load_groups(wb[c][:], wqb_words[:, :, 2 * BANK * c : 2 * BANK * (c + 1), :])
-        load_groups(wk[:, :, HALF:], wkva_words[:, :, HALF - ROPE : KV_LORA, :])
+        for c in range(2):
+            load_groups(wb[c][:], wqb_words[:, :, 3 * BANK * c : 3 * BANK * (c + 1), :])
 
         turned = {}
         acc = {}
@@ -127,12 +124,11 @@ def tile_mlaselfattn_w8_kernel(
         xv = {}
         xw = {}
         xi = {}
-        planes = {}
 
         def codes_of(i, g):
             if i < 2:
                 return xb_early[g // 2][:, i, 512 * (g % 2) : 512 * (g % 2 + 1)].bitcast(FP8)
-            return xb_late[:, i - 2, 512 * g : 512 * (g + 1)].bitcast(FP8)
+            return xb_late[i - 2][:, 512 * g : 512 * (g + 1)].bitcast(FP8)
 
         def cast(i, g):
             xv[(i, g)] = kept("xv%d_%d" % (i, g), [P, 512], BF16)
@@ -167,17 +163,6 @@ def tile_mlaselfattn_w8_kernel(
                 in1=kscale[:, g, :].rearrange("p (u e) -> p u e", e=2).unsqueeze(1).to_broadcast([P, P, 2, 2]),
                 op=MULT,
             )
-
-        def scale_planes(g):
-            planes[g] = kept("planes%d" % g, [P, 2, 4, P], BF16)
-            values = turned[(2, g)].bitcast(BF16).rearrange("p j u (r e) -> p j u r e", e=2)
-            for t in range(4):
-                nc.scalar.activation(
-                    out=planes[g][:, :, t, :], in_=values[:, :, t // 2, :, t % 2], func=COPY, scale=kscale[:, g, t : t + 1]
-                )
-
-        def weave(i, g):
-            nc.vector.tensor_copy(out=xg[i][:, g, :, :], in_=planes[g][:, i - 2, :, :].rearrange("p t r -> p r t"))
 
         def gather_x(first, g):
             xi[(first, g)] = kept("xi%d_%d" % (first, g), [P, 2, P, 2], F32)
@@ -255,8 +240,10 @@ def tile_mlaselfattn_w8_kernel(
                 )
 
         def order_kv_scales():
-            nc.vector.tensor_copy(out=sk[:, 0:ROPE].bitcast(I32), in_=sk_raw[:, KV_LORA:].bitcast(I32))
-            nc.vector.tensor_copy(out=sk[:, ROPE:].bitcast(I32), in_=sk_raw[:, 0:KV_LORA].bitcast(I32))
+            nc.vector.tensor_copy(out=sk[:, 0:ROPE].bitcast(I32), in_=sk[:, KV_COLS:].bitcast(I32))
+
+        def order_kv_words():
+            nc.vector.tensor_copy(out=wk[:, :, 0:ROPE].bitcast(I32), in_=wk[:, :, KV_COLS:].bitcast(I32))
 
         def make_factors():
             h = ROPE // 2
@@ -286,7 +273,7 @@ def tile_mlaselfattn_w8_kernel(
             tiles = slice(first, first + 2)
             for j in range(2):
                 kv_group(first + j, 0, bank[:, j, :])
-            front = work.tile([P, 2, HALF], F32, name="front")
+            front = work.tile([P, 2, HALF], F32, name="fronts")
             terms = rope_terms(bank[:, :, 0:ROPE], factors[:, tiles, :, :].rearrange("p i j d -> p j i d"))
             nc.scalar.copy(out=front[:, :, ROPE:], in_=bank[:, :, ROPE:])
             rope_sum(front[:, :, 0:ROPE], terms)
@@ -299,36 +286,34 @@ def tile_mlaselfattn_w8_kernel(
             nc.scalar.copy(out=back[:], in_=bank[:, 0:HALF])
             nc.sync.dma_start(out=out_rows[:, i, Q_COLS + HALF :], in_=back[:])
 
-        def q_banks(i, first, banks):
-            tiles = [bank_tile(b) for b in banks]
-            for g in range(QG):
-                for j, bank in enumerate(tiles):
-                    n = first + j
-                    nc.tensor.matmul_mx(
-                        out=bank[:],
-                        lhsT=qc[i][:, g, :].bitcast(FP8X4),
-                        lhsT_scale=qs[i][:, g, :],
-                        rhs=wb[n // 2][:, g, BANK * (n % 2) : BANK * (n % 2 + 1)].bitcast(FP8X4),
-                        rhs_scale=sb[4 * g : P, BANK * n : BANK * (n + 1)],
-                        start=(g == 0),
-                        stop=(g == QG - 1),
-                    )
-            return tiles
+        def q_pass(i, n, g, bank):
+            nc.tensor.matmul_mx(
+                out=bank[:],
+                lhsT=qc[i][:, g, :].bitcast(FP8X4),
+                lhsT_scale=qs[i][:, g, :],
+                rhs=wb[n // 3][:, g, BANK * (n % 3) : BANK * (n % 3 + 1)].bitcast(FP8X4),
+                rhs_scale=sb[4 * g : P, BANK * n : BANK * (n + 1)],
+                start=(g == 0),
+                stop=(g == QG - 1),
+            )
 
         def q_part(i, first, banks):
             n = len(banks)
-            q = work.tile([P, n, BANK], F32, name="q%d" % n, bufs=6)
+            q = work.tile([P, n, BANK], F32, name="q%d" % n, bufs=4 * n - 2)
             sums = []
-            for j, whole in enumerate(q_banks(i, first, banks)):
+            for j, b in enumerate(banks):
+                whole = bank_tile(b)
+                for g in range(QG):
+                    q_pass(i, first + j, g, whole)
                 bank = whole[:].rearrange("p (b c) -> p b c", c=ROPE)
                 blocks = q[:, j, :].rearrange("p (b c) -> p b c", c=ROPE)
                 turning = (2 - 8 * (first + j)) % 3
                 h = len(range(turning, 8, 3))
                 terms = rope_terms(bank[:, turning::3, :], factors[:, i, :, :].unsqueeze(2).to_broadcast([P, 2, h, ROPE]))
-                sums.append((blocks[:, turning::3, :], terms))
                 for r in range(3):
                     if r != turning:
                         nc.scalar.copy(out=blocks[:, r::3, :], in_=bank[:, r::3, :])
+                sums.append((blocks[:, turning::3, :], terms))
             for target, terms in sums:
                 rope_sum(target, terms)
             nc.sync.dma_start(
@@ -348,73 +333,62 @@ def tile_mlaselfattn_w8_kernel(
         turn(2, [(0, 2), (1, 2)])
         turn(3, [(0, 3), (1, 3)])
         widen(0, 0)
-        cast_sorted(2, 0)
-        cast(3, 0)
-        cast_sorted(2, 1)
-        cast(3, 1)
-        cast_sorted(2, 2)
-        cast(3, 2)
-        cast_sorted(2, 3)
-        cast(3, 3)
+        for g in range(XG):
+            cast(2, g)
+            cast_sorted(3, g)
         turn(4, [(2, 0), (3, 0)])
         keep_warm(idle, 1)
         turn(5, [(2, 1), (3, 1)])
         turn(6, [(2, 2), (3, 2)])
         turn(7, [(2, 3), (3, 3)])
-        gather_x(0, 2)
-        gather_x(0, 3)
-        gather_x(2, 0)
-        gather_x(2, 1)
-        scale_planes(2)
-        scale_planes(3)
+        for first, g in ((2, 0), (2, 1), (0, 2), (0, 3), (2, 2), (2, 3)):
+            gather_x(first, g)
         quant_x(0, 0, 1)
         widen(1, 0)
         widen(0, 1)
         quant_x(1, 0, 1)
         widen(1, 1)
         quant_x(0, 1, 1)
-        scale_x(0, 2)
-        quant_x(1, 1, 1)
-        scale_x(1, 2)
-        quant_x(0, 2, 1)
-        scale_x(0, 3)
-        quant_x(1, 2, 1)
-        scale_x(1, 3)
-        quant_x(0, 3, 1)
-        nc.vector.memset(sb[:, 0:64].bitcast(I32), 0)
-        load_planes(sb, wqb_scales, nc.gpsimd)
-        scale_x(2, 0)
-        quant_x(1, 3, 1)
-        scale_x(2, 1)
-        weave(2, 2)
-        quant_x(2, 0, 2)
-        weave(2, 3)
-        weave(3, 2)
-        quant_x(2, 2, 2)
-        weave(3, 3)
-        scale_x(3, 0)
-        quant_x(3, 2, 2)
+        behind = (1, 1)
+        for unit in [(2, 0), (2, 1)] + [(i, g) for g in (2, 3) for i in range(3)] + [(3, 0)]:
+            scale_x(*unit)
+            quant_x(*behind, 1)
+            behind = unit
+            if unit == (0, 3):
+                nc.vector.memset(sb[:, 0:64].bitcast(I32), 0)
+                load_planes(sb[:], wqb_scales, nc.gpsimd)
         scale_x(3, 1)
-        make_factors()
+        scale_x(3, 2)
         quant_x(3, 0, 2)
+        scale_x(3, 3)
         order_kv_scales()
-        banks = ((0, 2), (3, 1), (4, 5))
+        quant_x(3, 2, 2)
+        order_kv_words()
+        make_factors()
+        banks = ((0, 4, 6), (5, 1, 7), (2, 3))
         for g, first, count in pieces:
-            for i in range(2):
+            for i in range(3):
                 for n in range(first, first + count):
-                    qa_pass(i, g, n, banks[n][i])
+                    if i < 2 or (n < 2 and g >= 2):
+                        qa_pass(i, g, n, banks[n][i])
+            if (g, first) == (1, 2):
+                for early in range(2):
+                    for n in range(2):
+                        qa_pass(2, early, n, banks[n][2])
         for n in range(QG):
-            for i in range(2):
+            for i in range(len(banks[n])):
                 round_qa(i, n)
-        for i, three in ((2, (6, 7, 0)), (3, (2, 3, 1))):
-            for g in range(XG):
-                for n in range(QG):
-                    qa_pass(i, g, n, three[n])
-            for n in range(QG):
-                round_qa(i, n)
-        kv_fronts(4, 0)
+        for g in range(XG):
+            qa_pass(2, g, 2, 0)
+        round_qa(2, 2)
+        for g in range(XG):
+            for n, b in enumerate((4, 6, 5)):
+                qa_pass(3, g, n, b)
+        for n in range(QG):
+            round_qa(3, n)
+        kv_fronts(1, 0)
         units = [(i, g) for i in range(TILES) for g in range(QG)]
-        for j, b in enumerate((5, 6, 7, 0, 2, 3)):
+        for j, b in enumerate((7, 2, 3, 0, 4, 6)):
             bank = bank_tile(b)
             for k in range(2):
                 i, g = units[2 * j + k]
@@ -425,13 +399,13 @@ def tile_mlaselfattn_w8_kernel(
             if i:
                 quant_qa(i - 1)
         quant_qa(TILES - 1)
-        kv_fronts(1, 2)
-        pairs = ((4, 5), (6, 7), (0, 2), (3, 1))
+        kv_fronts(5, 2)
+        pairs = ((1, 7), (2, 3), (0, 4), (6, 5))
         for n in range(0, 6, 2):
             for i in range(TILES):
                 if (i, n) != (3, 4):
                     q_part(i, n, pairs[i])
-        q_part(3, 4, (3,))
-        q_part(3, 5, (1,))
-        for i, b in enumerate((4, 5, 6, 7)):
+        q_part(3, 4, (6,))
+        q_part(3, 5, (5,))
+        for i, b in enumerate((1, 7, 2, 3)):
             kv_back(b, i)

@@ -20,6 +20,7 @@ FP8 = mybir.dt.float8_e4m3fn
 FP8X4 = mybir.dt.float8_e4m3fn_x4
 MULT = mybir.AluOpType.mult
 ADD = mybir.AluOpType.add
+COPY = mybir.ActivationFunctionType.Copy
 
 P = 128
 BANK = 512
@@ -53,9 +54,9 @@ def tile_mlaselfattn_w8_kernel(
         xc = [kept("xc%d" % i, [P, XG, P], U32) for i in range(TILES)]
         xs = [kept("xs%d" % i, [P, XG, P], U8) for i in range(TILES)]
         qv = [kept("qv%d" % i, [P, QG, BANK], BF16) for i in range(TILES)]
-        qg = [kept("qg%d" % i, [P, QG, P, 4], BF16) for i in range(TILES)]
-        qc = [kept("qc%d" % i, [P, QG, P], U32) for i in range(TILES)]
-        qs = [kept("qs%d" % i, [P, QG, P], U8) for i in range(TILES)]
+        qg = [kept("qg%d" % j, [P, 2, P, 4], BF16) for j in range(6)]
+        qc = [kept("qc%d" % j, [P, 2, P], U32) for j in range(6)]
+        qs = [kept("qs%d" % j, [P, 2, P], U8) for j in range(6)]
         wb = [kept("wb%d" % c, [P, QG, 3 * BANK], U32) for c in range(2)]
         wk = kept("wk", [P, XG, ROPE + KV_COLS], U32)
         sa = kept("sa", [P, Q_LORA], U8)
@@ -80,8 +81,8 @@ def tile_mlaselfattn_w8_kernel(
 
         ctx.enter_context(tc.manual_schedule())
 
-        nc.vector.memset(sa[:].bitcast(I32), 0)
         nc.vector.memset(zeros[:].bitcast(I32), 0)
+        nc.vector.memset(sa[:].bitcast(I32), 0)
         nc.vector.memset(warm[:], 0.0)
         nc.vector.memset(one[:], 1.0)
         nc.vector.memset(sb[:, 64:].bitcast(I32), 0)
@@ -124,6 +125,7 @@ def tile_mlaselfattn_w8_kernel(
         xv = {}
         xw = {}
         xi = {}
+        planes = {}
 
         def codes_of(i, g):
             if i < 2:
@@ -163,6 +165,16 @@ def tile_mlaselfattn_w8_kernel(
                 in1=kscale[:, g, :].rearrange("p (u e) -> p u e", e=2).unsqueeze(1).to_broadcast([P, P, 2, 2]),
                 op=MULT,
             )
+
+        def scale_planes(i, g):
+            planes[(i, g)] = kept("xv2_%d" % g, [P, 4, P], BF16)
+            for t in range(4):
+                nc.scalar.activation(
+                    out=planes[(i, g)][:, t, :], in_=gathered(i, g)[:, :, t], func=COPY, scale=kscale[:, g, t : t + 1]
+                )
+
+        def weave(i, g):
+            nc.vector.tensor_copy(out=xg[i][:, g, :, :], in_=planes[(i, g)][:].rearrange("p t r -> p r t"))
 
         def gather_x(first, g):
             xi[(first, g)] = kept("xi%d_%d" % (first, g), [P, 2, P, 2], F32)
@@ -208,23 +220,26 @@ def tile_mlaselfattn_w8_kernel(
                 in_=acc[(i, n)][:].rearrange("p (q u e) -> p u q e", u=2, e=2),
             )
 
-        def turn_qa(i, g, half):
-            words = qv[i][:, g, :].bitcast(F32)
-            for u in range(2):
-                nc.tensor.transpose(half[:, P * u : P * (u + 1)], words[:, P * u : P * (u + 1)], ident[:])
-            turned[("qa", i, g)] = half
+        def turn_qa(j, b):
+            bank = bank_tile(b)[:].rearrange("p (k u r) -> p k u r", k=2, u=2)
+            for k in range(2):
+                i, g = divmod(2 * j + k, QG)
+                words = qv[i][:, g, :].bitcast(F32)
+                for u in range(2):
+                    nc.tensor.transpose(bank[:, k, u, :], words[:, P * u : P * (u + 1)], ident[:])
+            turned[("qa", j)] = bank
 
-        def gather_qa(i, g):
+        def gather_qa(j):
             nc.scalar.copy(
-                out=qg[i][:, g, :, :].rearrange("p r t -> p (r t)").bitcast(F32).rearrange("p (r u) -> p r u", u=2),
-                in_=turned[("qa", i, g)].rearrange("p (u r) -> p r u", u=2),
+                out=qg[j][:].rearrange("p k r t -> p (k r t)").bitcast(F32).rearrange("p (k r u) -> p k r u", k=2, u=2),
+                in_=turned[("qa", j)].rearrange("p k u r -> p k r u"),
             )
 
-        def quant_qa(i):
+        def quant_qa(j):
             nc.vector.quantize_mx(
-                out=qc[i][:].rearrange("p g r -> p (g r)").bitcast(FP8X4),
-                scales=qs[i][:].rearrange("p g r -> p (g r)"),
-                in_=qg[i][:].rearrange("p g r t -> p (g r t)"),
+                out=qc[j][:].rearrange("p k r -> p (k r)").bitcast(FP8X4),
+                scales=qs[j][:].rearrange("p k r -> p (k r)"),
+                in_=qg[j][:].rearrange("p k r t -> p (k r t)"),
             )
 
         def kv_group(i, first, target):
@@ -270,14 +285,18 @@ def tile_mlaselfattn_w8_kernel(
 
         def kv_fronts(b, first):
             bank = bank_tile(b)[:].rearrange("p (j c) -> p j c", j=2)
-            tiles = slice(first, first + 2)
             for j in range(2):
                 kv_group(first + j, 0, bank[:, j, :])
+            return bank
+
+        def rotate_fronts(bank, first):
             front = work.tile([P, 2, HALF], F32, name="fronts")
-            terms = rope_terms(bank[:, :, 0:ROPE], factors[:, tiles, :, :].rearrange("p i j d -> p j i d"))
+            terms = rope_terms(bank[:, :, 0:ROPE], factors[:, first : first + 2, :, :].rearrange("p i j d -> p j i d"))
+            return front, terms
+
+        def store_fronts(bank, first, front):
             nc.scalar.copy(out=front[:, :, ROPE:], in_=bank[:, :, ROPE:])
-            rope_sum(front[:, :, 0:ROPE], terms)
-            nc.sync.dma_start(out=out_rows[:, tiles, Q_COLS : Q_COLS + HALF], in_=front[:])
+            nc.sync.dma_start(out=out_rows[:, first : first + 2, Q_COLS : Q_COLS + HALF], in_=front[:])
 
         def kv_back(b, i):
             bank = bank_tile(b)
@@ -287,10 +306,11 @@ def tile_mlaselfattn_w8_kernel(
             nc.sync.dma_start(out=out_rows[:, i, Q_COLS + HALF :], in_=back[:])
 
         def q_pass(i, n, g, bank):
+            j, k = divmod(QG * i + g, 2)
             nc.tensor.matmul_mx(
                 out=bank[:],
-                lhsT=qc[i][:, g, :].bitcast(FP8X4),
-                lhsT_scale=qs[i][:, g, :],
+                lhsT=qc[j][:, k, :].bitcast(FP8X4),
+                lhsT_scale=qs[j][:, k, :],
                 rhs=wb[n // 3][:, g, BANK * (n % 3) : BANK * (n % 3 + 1)].bitcast(FP8X4),
                 rhs_scale=sb[4 * g : P, BANK * n : BANK * (n + 1)],
                 start=(g == 0),
@@ -299,7 +319,7 @@ def tile_mlaselfattn_w8_kernel(
 
         def q_part(i, first, banks):
             n = len(banks)
-            q = work.tile([P, n, BANK], F32, name="q%d" % n, bufs=4 * n - 2)
+            q = work.tile([P, n, BANK], F32, name="q%d" % n, bufs=4)
             sums = []
             for j, b in enumerate(banks):
                 whole = bank_tile(b)
@@ -343,6 +363,8 @@ def tile_mlaselfattn_w8_kernel(
         turn(7, [(2, 3), (3, 3)])
         for first, g in ((2, 0), (2, 1), (0, 2), (0, 3), (2, 2), (2, 3)):
             gather_x(first, g)
+        for g in range(XG):
+            scale_planes(3, g)
         quant_x(0, 0, 1)
         widen(1, 0)
         widen(0, 1)
@@ -350,17 +372,19 @@ def tile_mlaselfattn_w8_kernel(
         widen(1, 1)
         quant_x(0, 1, 1)
         behind = (1, 1)
-        for unit in [(2, 0), (2, 1)] + [(i, g) for g in (2, 3) for i in range(3)] + [(3, 0)]:
+        for unit in [(2, 0), (2, 1)] + [(i, g) for g in (2, 3) for i in range(3)]:
             scale_x(*unit)
             quant_x(*behind, 1)
             behind = unit
             if unit == (0, 3):
                 nc.vector.memset(sb[:, 0:64].bitcast(I32), 0)
                 load_planes(sb[:], wqb_scales, nc.gpsimd)
-        scale_x(3, 1)
-        scale_x(3, 2)
+        weave(3, 0)
+        quant_x(2, 3, 1)
+        weave(3, 1)
+        weave(3, 2)
         quant_x(3, 0, 2)
-        scale_x(3, 3)
+        weave(3, 3)
         order_kv_scales()
         quant_x(3, 2, 2)
         order_kv_words()
@@ -381,31 +405,29 @@ def tile_mlaselfattn_w8_kernel(
         for g in range(XG):
             qa_pass(2, g, 2, 0)
         round_qa(2, 2)
-        for g in range(XG):
-            for n, b in enumerate((4, 6, 5)):
+        for n, b in enumerate((4, 6, 5)):
+            for g in range(XG):
                 qa_pass(3, g, n, b)
-        for n in range(QG):
             round_qa(3, n)
-        kv_fronts(1, 0)
-        units = [(i, g) for i in range(TILES) for g in range(QG)]
+        early = kv_fronts(1, 0)
+        early_front, terms = rotate_fronts(early, 0)
         for j, b in enumerate((7, 2, 3, 0, 4, 6)):
-            bank = bank_tile(b)
-            for k in range(2):
-                i, g = units[2 * j + k]
-                turn_qa(i, g, bank[:, HALF * k : HALF * (k + 1)])
-        for i in range(TILES):
-            for g in range(QG):
-                gather_qa(i, g)
-            if i:
-                quant_qa(i - 1)
-        quant_qa(TILES - 1)
-        kv_fronts(5, 2)
-        pairs = ((1, 7), (2, 3), (0, 4), (6, 5))
-        for n in range(0, 6, 2):
+            turn_qa(j, b)
+        late = kv_fronts(5, 2)
+        rope_sum(early_front[:, :, 0:ROPE], terms)
+        for j in range(6):
+            gather_qa(j)
+            quant_qa(j)
+            if j == 2:
+                store_fronts(early, 0, early_front)
+        late_front, terms = rotate_fronts(late, 2)
+        rope_sum(late_front[:, :, 0:ROPE], terms)
+        store_fronts(late, 2, late_front)
+        ring = (7, 2, 3, 1, 0, 4, 6, 5)
+        used = 0
+        for first, count in ((0, 3), (4, 2), (3, 1)):
             for i in range(TILES):
-                if (i, n) != (3, 4):
-                    q_part(i, n, pairs[i])
-        q_part(3, 4, (6,))
-        q_part(3, 5, (5,))
-        for i, b in enumerate((1, 7, 2, 3)):
-            kv_back(b, i)
+                q_part(i, first, [ring[(used + j) % 8] for j in range(count)])
+                used = used + count
+        for i in range(TILES):
+            kv_back(ring[i], i)

@@ -57,7 +57,7 @@ def tile_mlaselfattn_w8_kernel(
         qg = [kept("qg%d" % j, [P, 2, P, 4], BF16) for j in range(6)]
         qc = [kept("qc%d" % j, [P, 2, P], U32) for j in range(6)]
         qs = [kept("qs%d" % j, [P, 2, P], U8) for j in range(6)]
-        wb = [kept("wb%d" % c, [P, QG, 3 * BANK], U32) for c in range(2)]
+        wb = [kept("wb%d" % c, [P, QG, 2 * BANK], U32) for c in range(3)]
         wk = kept("wk", [P, XG, ROPE + KV_COLS], U32)
         sa = kept("sa", [P, Q_LORA], U8)
         sb = kept("sb", [P, Q_COLS], U8)
@@ -81,11 +81,11 @@ def tile_mlaselfattn_w8_kernel(
 
         ctx.enter_context(tc.manual_schedule())
 
-        nc.vector.memset(zeros[:].bitcast(I32), 0)
         nc.vector.memset(sa[:].bitcast(I32), 0)
+        nc.vector.memset(zeros[:].bitcast(I32), 0)
         nc.vector.memset(warm[:], 0.0)
         nc.vector.memset(one[:], 1.0)
-        nc.vector.memset(sb[:, 64:].bitcast(I32), 0)
+        nc.vector.memset(sb[:].bitcast(I32), 0)
         nc.vector.memset(sk[:, ROPE:].bitcast(I32), 0)
         make_identity(nc, ident[:])
 
@@ -95,10 +95,10 @@ def tile_mlaselfattn_w8_kernel(
         def load_groups(tile, words):
             nc.sync.dma_start(out=tile.bitcast(I32), in_=words.rearrange("g p n t -> p g (n t)").bitcast(I32))
 
-        def load_planes(tile, scales, queue):
+        def load_planes(tile, scales):
             groups = scales.shape[0]
             for q in range(4):
-                queue.dma_start(
+                nc.sync.dma_start(
                     out=tile[32 * q : 32 * q + 4 * groups].bitcast(I32),
                     in_=scales[:, 4 * q : 4 * q + 4, :].bitcast(I32),
                 )
@@ -109,15 +109,16 @@ def tile_mlaselfattn_w8_kernel(
         for j in range(2):
             nc.sync.dma_start(out=xb_late[j][:], in_=x_rows[:, 2 + j, :])
         nc.scalar.copy(out=warm[:, 4:8], in_=warm[:, 0:4])
-        load_planes(sa[:], wqa_scales, nc.sync)
+        load_planes(sa[:], wqa_scales)
         for g, first, count in pieces:
             load_words(wa[("piece", g, first)][:], wqa_words[g, :, BANK * first : BANK * (first + count), :])
-        load_planes(sk[:, ROPE:], wkva_scales, nc.sync)
+        load_planes(sk[:, ROPE:], wkva_scales)
         load_groups(wk[:, :, ROPE:], wkva_words)
         nc.sync.dma_start(out=cos_sb[:], in_=cos.rearrange("b (q i) d -> (b q) i d", i=TILES))
         nc.sync.dma_start(out=sin_sb[:], in_=sin.rearrange("b (q i) d -> (b q) i d", i=TILES))
-        for c in range(2):
-            load_groups(wb[c][:], wqb_words[:, :, 3 * BANK * c : 3 * BANK * (c + 1), :])
+        load_planes(sb[:], wqb_scales)
+        for c in range(3):
+            load_groups(wb[c][:], wqb_words[:, :, 2 * BANK * c : 2 * BANK * (c + 1), :])
 
         turned = {}
         acc = {}
@@ -311,7 +312,7 @@ def tile_mlaselfattn_w8_kernel(
                 out=bank[:],
                 lhsT=qc[j][:, k, :].bitcast(FP8X4),
                 lhsT_scale=qs[j][:, k, :],
-                rhs=wb[n // 3][:, g, BANK * (n % 3) : BANK * (n % 3 + 1)].bitcast(FP8X4),
+                rhs=wb[n // 2][:, g, BANK * (n % 2) : BANK * (n % 2 + 1)].bitcast(FP8X4),
                 rhs_scale=sb[4 * g : P, BANK * n : BANK * (n + 1)],
                 start=(g == 0),
                 stop=(g == QG - 1),
@@ -376,9 +377,6 @@ def tile_mlaselfattn_w8_kernel(
             scale_x(*unit)
             quant_x(*behind, 1)
             behind = unit
-            if unit == (0, 3):
-                nc.vector.memset(sb[:, 0:64].bitcast(I32), 0)
-                load_planes(sb[:], wqb_scales, nc.gpsimd)
         weave(3, 0)
         quant_x(2, 3, 1)
         weave(3, 1)

@@ -28,6 +28,7 @@ TILES = TOKENS // P
 XG = HIDDEN // 512
 QG = Q_LORA // 512
 HALF = BANK // 2
+PLANES = ((2, 2), (2, 3), (3, 0), (3, 1), (3, 2), (3, 3))
 
 
 def tile_mlaselfattn_w8_kernel(
@@ -168,7 +169,7 @@ def tile_mlaselfattn_w8_kernel(
             )
 
         def scale_planes(i, g):
-            planes[(i, g)] = kept("xv2_%d" % g, [P, 4, P], BF16)
+            planes[(i, g)] = kept("xv%d_%d" % (i - 1, g), [P, 4, P], BF16)
             for t in range(4):
                 nc.scalar.activation(
                     out=planes[(i, g)][:, t, :], in_=gathered(i, g)[:, :, t], func=COPY, scale=kscale[:, g, t : t + 1]
@@ -364,17 +365,22 @@ def tile_mlaselfattn_w8_kernel(
         turn(7, [(2, 3), (3, 3)])
         for first, g in ((2, 0), (2, 1), (0, 2), (0, 3), (2, 2), (2, 3)):
             gather_x(first, g)
-        for g in range(XG):
-            scale_planes(3, g)
+        for unit in PLANES:
+            scale_planes(*unit)
         quant_x(0, 0, 1)
         widen(1, 0)
         widen(0, 1)
         quant_x(1, 0, 1)
         widen(1, 1)
         quant_x(0, 1, 1)
-        behind = (1, 1)
-        for unit in [(2, 0), (2, 1)] + [(i, g) for g in (2, 3) for i in range(3)]:
-            scale_x(*unit)
+        quant_x(1, 1, 1)
+        scale_x(2, 0)
+        behind = (2, 0)
+        for unit in [(2, 1)] + [(i, g) for g in (2, 3) for i in range(3)]:
+            if unit in PLANES:
+                weave(*unit)
+            else:
+                scale_x(*unit)
             quant_x(*behind, 1)
             behind = unit
         weave(3, 0)
@@ -387,7 +393,7 @@ def tile_mlaselfattn_w8_kernel(
         quant_x(3, 2, 2)
         order_kv_words()
         make_factors()
-        banks = ((0, 4, 6), (5, 1, 7), (2, 3))
+        banks = ((0, 5, 6), (4, 1, 7), (2, 3))
         for g, first, count in pieces:
             for i in range(3):
                 for n in range(first, first + count):
@@ -397,21 +403,20 @@ def tile_mlaselfattn_w8_kernel(
                 for early in range(2):
                     for n in range(2):
                         qa_pass(2, early, n, banks[n][2])
-        for n in range(QG):
-            for i in range(len(banks[n])):
-                round_qa(i, n)
+        for i, n in ((0, 0), (0, 1), (1, 0), (1, 1), (2, 0), (2, 1), (0, 2), (1, 2)):
+            round_qa(i, n)
         for g in range(XG):
             qa_pass(2, g, 2, 0)
         round_qa(2, 2)
-        for n, b in enumerate((4, 6, 5)):
+        for n, b in enumerate((4, 5, 6)):
             for g in range(XG):
                 qa_pass(3, g, n, b)
             round_qa(3, n)
         early = kv_fronts(1, 0)
         early_front, terms = rotate_fronts(early, 0)
-        for j, b in enumerate((7, 2, 3, 0, 4, 6)):
+        for j, b in enumerate((7, 2, 3, 0, 4, 5)):
             turn_qa(j, b)
-        late = kv_fronts(5, 2)
+        late = kv_fronts(6, 2)
         rope_sum(early_front[:, :, 0:ROPE], terms)
         for j in range(6):
             gather_qa(j)
@@ -421,7 +426,7 @@ def tile_mlaselfattn_w8_kernel(
         late_front, terms = rotate_fronts(late, 2)
         rope_sum(late_front[:, :, 0:ROPE], terms)
         store_fronts(late, 2, late_front)
-        ring = (7, 2, 3, 1, 0, 4, 6, 5)
+        ring = (7, 2, 3, 1, 0, 4, 5, 6)
         used = 0
         for first, count in ((0, 3), (4, 2), (3, 1)):
             for i in range(TILES):

@@ -28,6 +28,7 @@ TILES = TOKENS // P
 XG = HIDDEN // 512
 QG = Q_LORA // 512
 HALF = BANK // 2
+WB_PIECES = ((0, 2), (2, 1), (4, 2), (3, 1))
 PLANES = ((2, 2), (2, 3), (3, 0), (3, 1), (3, 2), (3, 3))
 
 
@@ -58,7 +59,12 @@ def tile_mlaselfattn_w8_kernel(
         qg = [kept("qg%d" % j, [P, 2, P, 4], BF16) for j in range(6)]
         qc = [kept("qc%d" % j, [P, 2, P], U32) for j in range(6)]
         qs = [kept("qs%d" % j, [P, 2, P], U8) for j in range(6)]
-        wb = [kept("wb%d" % c, [P, QG, 2 * BANK], U32) for c in range(3)]
+        wb = {}
+        for first, count in WB_PIECES:
+            piece = kept("wb%d" % first, [P, QG, count * BANK], U32)
+            wb[("piece", first)] = piece
+            for n in range(count):
+                wb[first + n] = piece[:, :, BANK * n : BANK * (n + 1)]
         wk = kept("wk", [P, XG, ROPE + KV_COLS], U32)
         sa = kept("sa", [P, Q_LORA], U8)
         sb = kept("sb", [P, Q_COLS], U8)
@@ -72,13 +78,14 @@ def tile_mlaselfattn_w8_kernel(
         warm = kept("warm", [P, 8], F32)
         zeros = kept("zeros", [P, BANK], BF16)
 
-        pieces = [(0, 0, 2), (1, 0, 2), (0, 2, 1), (1, 2, 1), (2, 0, 3), (3, 0, 2), (3, 2, 1)]
+        pieces = [(0, 1, 0, 2), (1, 1, 0, 2), (0, 2, 2, 1), (2, 1, 0, 3), (3, 1, 0, 3)]
         wa = {}
-        for g, first, count in pieces:
-            piece = kept("wa%d_%d" % (g, first), [P, count * BANK], U32)
+        for g, groups, first, count in pieces:
+            piece = kept("wa%d_%d" % (g, first), [P, groups, count * BANK], U32)
             wa[("piece", g, first)] = piece
-            for n in range(count):
-                wa[(g, first + n)] = piece[:, BANK * n : BANK * (n + 1)]
+            for j in range(groups):
+                for n in range(count):
+                    wa[(g + j, first + n)] = piece[:, j, BANK * n : BANK * (n + 1)]
 
         ctx.enter_context(tc.manual_schedule())
 
@@ -89,9 +96,6 @@ def tile_mlaselfattn_w8_kernel(
         nc.vector.memset(sb[:].bitcast(I32), 0)
         nc.vector.memset(sk[:, ROPE:].bitcast(I32), 0)
         make_identity(nc, ident[:])
-
-        def load_words(tile, words):
-            nc.sync.dma_start(out=tile.bitcast(I32), in_=words.rearrange("p n t -> p (n t)").bitcast(I32))
 
         def load_groups(tile, words):
             nc.sync.dma_start(out=tile.bitcast(I32), in_=words.rearrange("g p n t -> p g (n t)").bitcast(I32))
@@ -111,15 +115,15 @@ def tile_mlaselfattn_w8_kernel(
             nc.sync.dma_start(out=xb_late[j][:], in_=x_rows[:, 2 + j, :])
         nc.scalar.copy(out=warm[:, 4:8], in_=warm[:, 0:4])
         load_planes(sa[:], wqa_scales)
-        for g, first, count in pieces:
-            load_words(wa[("piece", g, first)][:], wqa_words[g, :, BANK * first : BANK * (first + count), :])
+        for g, groups, first, count in pieces:
+            load_groups(wa[("piece", g, first)][:], wqa_words[g : g + groups, :, BANK * first : BANK * (first + count), :])
         load_planes(sk[:, ROPE:], wkva_scales)
         load_groups(wk[:, :, ROPE:], wkva_words)
         nc.sync.dma_start(out=cos_sb[:], in_=cos.rearrange("b (q i) d -> (b q) i d", i=TILES))
         nc.sync.dma_start(out=sin_sb[:], in_=sin.rearrange("b (q i) d -> (b q) i d", i=TILES))
         load_planes(sb[:], wqb_scales)
-        for c in range(3):
-            load_groups(wb[c][:], wqb_words[:, :, 2 * BANK * c : 2 * BANK * (c + 1), :])
+        for first, count in WB_PIECES:
+            load_groups(wb[("piece", first)][:], wqb_words[:, :, BANK * first : BANK * (first + count), :])
 
         turned = {}
         acc = {}
@@ -313,7 +317,7 @@ def tile_mlaselfattn_w8_kernel(
                 out=bank[:],
                 lhsT=qc[j][:, k, :].bitcast(FP8X4),
                 lhsT_scale=qs[j][:, k, :],
-                rhs=wb[n // 2][:, g, BANK * (n % 2) : BANK * (n % 2 + 1)].bitcast(FP8X4),
+                rhs=wb[n][:, g, :].bitcast(FP8X4),
                 rhs_scale=sb[4 * g : P, BANK * n : BANK * (n + 1)],
                 start=(g == 0),
                 stop=(g == QG - 1),
@@ -394,7 +398,7 @@ def tile_mlaselfattn_w8_kernel(
         order_kv_words()
         make_factors()
         banks = ((0, 5, 6), (4, 1, 7), (2, 3))
-        for g, first, count in pieces:
+        for g, first, count in ((0, 0, 2), (1, 0, 2), (0, 2, 1), (1, 2, 1), (2, 0, 3), (3, 0, 2), (3, 2, 1)):
             for i in range(3):
                 for n in range(first, first + count):
                     if i < 2 or (n < 2 and g >= 2):

from contextlib import ExitStack

import concourse.mybir as mybir
from concourse.masks import make_identity

TOKENS, HIDDEN, Q_LORA = 512, 2048, 1536
HEADS, NOPE, ROPE, KV_LORA = 16, 128, 64, 448
HEAD = NOPE + ROPE
Q_COLS = HEADS * HEAD
KV_COLS = KV_LORA + ROPE

FLOPS = 2 * TOKENS * HIDDEN * (Q_LORA + KV_COLS) + 2 * TOKENS * Q_LORA * Q_COLS

F32 = mybir.dt.float32
BF16 = mybir.dt.bfloat16
I32 = mybir.dt.int32
U32 = mybir.dt.uint32
U8 = mybir.dt.uint8
FP8 = mybir.dt.float8_e4m3fn
FP8X4 = mybir.dt.float8_e4m3fn_x4
MULT = mybir.AluOpType.mult
ADD = mybir.AluOpType.add
COPY = mybir.ActivationFunctionType.Copy

P = 128
BANK = 512
TILES = TOKENS // P
XG = HIDDEN // 512
QG = Q_LORA // 512
HALF = BANK // 2
WB_PIECES = ((0, 2), (2, 1), (4, 2), (3, 1))
PLANES = ((2, 2), (2, 3), (3, 0), (3, 1), (3, 2), (3, 3))


def tile_mlaselfattn_w8_kernel(
    tc, x_bytes, x_scale, cos, sin, wqa_words, wqa_scales, wqb_words, wqb_scales, wkva_words, wkva_scales, out
):
    nc = tc.nc
    x_rows = x_bytes.rearrange("b (q i) k -> (b q) i k", i=TILES)
    out_rows = out.rearrange("b (q i) c -> (b q) i c", i=TILES)

    with ExitStack() as ctx:
        keep = ctx.enter_context(tc.tile_pool(name="keep", bufs=1))
        work = ctx.enter_context(tc.tile_pool(name="work", bufs=2))
        psum = ctx.enter_context(tc.psum_pool(name="psum", bufs=1))

        def bank_tile(b):
            return psum.tile([P, BANK], F32, name="bank%d" % b)

        def kept(name, shape, dtype):
            return keep.tile(shape, dtype, name=name, align_bytes=64)

        xb_early = [kept("xb_early%d" % h, [P, 2, HIDDEN // 2], U8) for h in range(2)]
        xb_late = [kept("xb_late%d" % j, [P, HIDDEN], U8) for j in range(2)]
        xg = [kept("xg%d" % i, [P, XG, P, 4], BF16) for i in range(TILES)]
        xc = [kept("xc%d" % i, [P, XG, P], U32) for i in range(TILES)]
        xs = [kept("xs%d" % i, [P, XG, P], U8) for i in range(TILES)]
        qv = [kept("qv%d" % i, [P, QG, BANK], BF16) for i in range(TILES)]
        qg = [kept("qg%d" % j, [P, 2, P, 4], BF16) for j in range(6)]
        qc = [kept("qc%d" % j, [P, 2, P], U32) for j in range(6)]
        qs = [kept("qs%d" % j, [P, 2, P], U8) for j in range(6)]
        wb = {}
        for first, count in WB_PIECES:
            piece = kept("wb%d" % first, [P, QG, count * BANK], U32)
            wb[("piece", first)] = piece
            for n in range(count):
                wb[first + n] = piece[:, :, BANK * n : BANK * (n + 1)]
        wk = kept("wk", [P, XG, ROPE + KV_COLS], U32)
        sa = kept("sa", [P, Q_LORA], U8)
        sb = kept("sb", [P, Q_COLS], U8)
        sk = kept("sk", [P, ROPE + KV_COLS], U8)
        kscale = kept("kscale", [P, XG, 4], F32)
        cos_sb = kept("cos_sb", [P, TILES, ROPE], BF16)
        sin_sb = kept("sin_sb", [P, TILES, ROPE], BF16)
        factors = kept("factors", [P, TILES, 2, ROPE], BF16)
        one = kept("one", [P, 8], F32)
        ident = kept("ident", [P, P], F32)
        warm = kept("warm", [P, 8], F32)
        zeros = kept("zeros", [P, BANK], BF16)

        pieces = [(0, 1, 0, 2), (1, 1, 0, 2), (0, 2, 2, 1), (2, 1, 0, 3), (3, 1, 0, 3)]
        wa = {}
        for g, groups, first, count in pieces:
            piece = kept("wa%d_%d" % (g, first), [P, groups, count * BANK], U32)
            wa[("piece", g, first)] = piece
            for j in range(groups):
                for n in range(count):
                    wa[(g + j, first + n)] = piece[:, j, BANK * n : BANK * (n + 1)]

        ctx.enter_context(tc.manual_schedule())

        nc.vector.memset(sa[:].bitcast(I32), 0)
        nc.vector.memset(zeros[:].bitcast(I32), 0)
        nc.vector.memset(warm[:], 0.0)
        nc.vector.memset(one[:], 1.0)
        nc.vector.memset(sb[:].bitcast(I32), 0)
        nc.vector.memset(sk[:, ROPE:].bitcast(I32), 0)
        make_identity(nc, ident[:])

        def load_groups(tile, words):
            nc.sync.dma_start(out=tile.bitcast(I32), in_=words.rearrange("g p n t -> p g (n t)").bitcast(I32))

        def load_planes(tile, scales):
            groups = scales.shape[0]
            for q in range(4):
                nc.sync.dma_start(
                    out=tile[32 * q : 32 * q + 4 * groups].bitcast(I32),
                    in_=scales[:, 4 * q : 4 * q + 4, :].bitcast(I32),
                )

        for h in range(2):
            nc.sync.dma_start(out=xb_early[h][:], in_=x_rows[:, 0:2, 1024 * h : 1024 * (h + 1)])
        nc.sync.dma_start(out=kscale[:], in_=x_scale.rearrange("a b (g p t) -> p (a b g) t", p=P, t=4))
        for j in range(2):
            nc.sync.dma_start(out=xb_late[j][:], in_=x_rows[:, 2 + j, :])
        nc.scalar.copy(out=warm[:, 4:8], in_=warm[:, 0:4])
        load_planes(sa[:], wqa_scales)
        for g, groups, first, count in pieces:
            load_groups(wa[("piece", g, first)][:], wqa_words[g : g + groups, :, BANK * first : BANK * (first + count), :])
        load_planes(sk[:, ROPE:], wkva_scales)
        load_groups(wk[:, :, ROPE:], wkva_words)
        nc.sync.dma_start(out=cos_sb[:], in_=cos.rearrange("b (q i) d -> (b q) i d", i=TILES))
        nc.sync.dma_start(out=sin_sb[:], in_=sin.rearrange("b (q i) d -> (b q) i d", i=TILES))
        load_planes(sb[:], wqb_scales)
        for first, count in WB_PIECES:
            load_groups(wb[("piece", first)][:], wqb_words[:, :, BANK * first : BANK * (first + count), :])

        turned = {}
        acc = {}

        xv = {}
        xw = {}
        xi = {}
        planes = {}

        def codes_of(i, g):
            if i < 2:
                return xb_early[g // 2][:, i, 512 * (g % 2) : 512 * (g % 2 + 1)].bitcast(FP8)
            return xb_late[i - 2][:, 512 * g : 512 * (g + 1)].bitcast(FP8)

        def cast(i, g):
            xv[(i, g)] = kept("xv%d_%d" % (i, g), [P, 512], BF16)
            nc.scalar.copy(out=xv[(i, g)][:], in_=codes_of(i, g))

        def cast_sorted(i, g):
            xw[(i, g)] = kept("xw%d_%d" % (i, g), [P, 2, P], F32)
            nc.vector.tensor_scalar(
                out=xw[(i, g)][:].bitcast(BF16).rearrange("p u (q e) -> p q u e", e=2),
                in0=codes_of(i, g).rearrange("p (q u e) -> p q u e", u=2, e=2),
                scalar1=one[:, 0:1],
                scalar2=None,
                op0=MULT,
            )

        def turn(b, units):
            bank = bank_tile(b)[:].rearrange("p (j u r) -> p j u r", j=2, u=2)
            for j, unit in enumerate(units):
                for u in range(2):
                    words = xw[unit][:, u, :] if unit in xw else xv[unit][:].bitcast(F32)[:, u:256:2]
                    nc.tensor.transpose(bank[:, j, u, :], words, ident[:])
            turned[units[0]] = bank

        def keep_warm(bank, n):
            for j in range(n):
                nc.tensor.matmul(bank[:], lhsT=zeros[:, 0:P], rhs=zeros[:], start=True, stop=True)

        def widen(i, g):
            nc.vector.tensor_tensor(
                out=xg[i][:, g, :, :].rearrange("p r (u e) -> p r u e", e=2),
                in0=turned[(i - i % 2, g)][:, i % 2, :, :].bitcast(BF16).rearrange("p u (r e) -> p r u e", e=2),
                in1=kscale[:, g, :].rearrange("p (u e) -> p u e", e=2).unsqueeze(1).to_broadcast([P, P, 2, 2]),
                op=MULT,
            )

        def scale_planes(i, g):
            planes[(i, g)] = kept("xv%d_%d" % (i - 1, g), [P, 4, P], BF16)
            for t in range(4):
                nc.scalar.activation(
                    out=planes[(i, g)][:, t, :], in_=gathered(i, g)[:, :, t], func=COPY, scale=kscale[:, g, t : t + 1]
                )

        def weave(i, g):
            nc.vector.tensor_copy(out=xg[i][:, g, :, :], in_=planes[(i, g)][:].rearrange("p t r -> p r t"))

        def gather_x(first, g):
            xi[(first, g)] = kept("xi%d_%d" % (first, g), [P, 2, P, 2], F32)
            nc.scalar.copy(out=xi[(first, g)][:], in_=turned[(first, g)].rearrange("p j u r -> p j r u"))

        def gathered(i, g):
            words = xi[(i - i % 2, g)][:, i % 2, :, :]
            return words.rearrange("p r u -> p (r u)").bitcast(BF16).rearrange("p (r t) -> p r t", t=4)

        def scale_x(i, g):
            nc.vector.tensor_tensor(
                out=xg[i][:, g, :, :],
                in0=gathered(i, g),
                in1=kscale[:, g, :].unsqueeze(1).to_broadcast([P, P, 4]),
                op=MULT,
            )

        def quant_x(i, g, n):
            gs = slice(g, g + n)
            nc.vector.quantize_mx(
                out=xc[i][:, gs, :].rearrange("p g r -> p (g r)").bitcast(FP8X4),
                scales=xs[i][:, gs, :].rearrange("p g r -> p (g r)"),
                in_=xg[i][:, gs, :, :].rearrange("p g r t -> p (g r t)"),
            )

        def qa_pass(i, g, n, b):
            if (i, n) not in acc:
                acc[(i, n)] = bank_tile(b)
            cols = slice(BANK * n, BANK * (n + 1))
            nc.tensor.matmul_mx(
                out=acc[(i, n)][:],
                lhsT=xc[i][:, g, :].bitcast(FP8X4),
                lhsT_scale=xs[i][:, g, :],
                rhs=wa[(g, n)].bitcast(FP8X4),
                rhs_scale=sa[4 * g : P, cols],
                start=(g == 0),
                stop=(g == XG - 1),
            )

        def round_qa(i, n):
            nc.scalar.copy(
                out=qv[i][:, n, :].rearrange("p (u q e) -> p u q e", u=2, e=2),
                in_=acc[(i, n)][:].rearrange("p (q u e) -> p u q e", u=2, e=2),
            )

        def turn_qa(j, b):
            bank = bank_tile(b)[:].rearrange("p (k u r) -> p k u r", k=2, u=2)
            for k in range(2):
                i, g = divmod(2 * j + k, QG)
                words = qv[i][:, g, :].bitcast(F32)
                for u in range(2):
                    nc.tensor.transpose(bank[:, k, u, :], words[:, P * u : P * (u + 1)], ident[:])
            turned[("qa", j)] = bank

        def gather_qa(j):
            nc.scalar.copy(
                out=qg[j][:].rearrange("p k r t -> p (k r t)").bitcast(F32).rearrange("p (k r u) -> p k r u", k=2, u=2),
                in_=turned[("qa", j)].rearrange("p k u r -> p k r u"),
            )

        def quant_qa(j):
            nc.vector.quantize_mx(
                out=qc[j][:].rearrange("p k r -> p (k r)").bitcast(FP8X4),
                scales=qs[j][:].rearrange("p k r -> p (k r)"),
                in_=qg[j][:].rearrange("p k r t -> p (k r t)"),
            )

        def kv_group(i, first, target):
            for g in range(XG):
                nc.tensor.matmul_mx(
                    out=target,
                    lhsT=xc[i][:, g, :].bitcast(FP8X4),
                    lhsT_scale=xs[i][:, g, :],
                    rhs=wk[:, g, first : first + HALF].bitcast(FP8X4),
                    rhs_scale=sk[4 * g : P, first : first + HALF],
                    start=(g == 0),
                    stop=(g == XG - 1),
                )

        def order_kv_scales():
            nc.vector.tensor_copy(out=sk[:, 0:ROPE].bitcast(I32), in_=sk[:, KV_COLS:].bitcast(I32))

        def order_kv_words():
            nc.vector.tensor_copy(out=wk[:, :, 0:ROPE].bitcast(I32), in_=wk[:, :, KV_COLS:].bitcast(I32))

        def make_factors():
            h = ROPE // 2
            nc.vector.tensor_copy(out=factors[:, :, 0, :], in_=cos_sb[:])
            nc.vector.tensor_copy(out=factors[:, :, 1, 0:h], in_=sin_sb[:, :, h:])
            nc.vector.tensor_scalar(out=factors[:, :, 1, h:], in0=sin_sb[:, :, 0:h], scalar1=-1.0, scalar2=None, op0=MULT)

        def rope_terms(pe, both):
            n = pe.shape[1]
            terms = work.tile([P, 2, 3, ROPE], F32, name="terms", bufs=4)
            nc.vector.tensor_tensor(
                out=terms[:, :, 0:n, :], in0=pe.unsqueeze(1).to_broadcast([P, 2, n, ROPE]), in1=both, op=MULT
            )
            return terms[:, :, 0:n, :]

        def rope_sum(target, terms):
            halves = terms.rearrange("p j b (s d) -> p j b s d", s=2)
            nc.vector.tensor_tensor(
                out=target.rearrange("p b (s d) -> p b s d", s=2),
                in0=halves[:, 0, :, :, :],
                in1=halves[:, 1, :, ::-1, :],
                op=ADD,
            )

        def kv_fronts(b, first):
            bank = bank_tile(b)[:].rearrange("p (j c) -> p j c", j=2)
            for j in range(2):
                kv_group(first + j, 0, bank[:, j, :])
            return bank

        def rotate_fronts(bank, first):
            front = work.tile([P, 2, HALF], F32, name="fronts")
            terms = rope_terms(bank[:, :, 0:ROPE], factors[:, first : first + 2, :, :].rearrange("p i j d -> p j i d"))
            return front, terms

        def store_fronts(bank, first, front):
            nc.scalar.copy(out=front[:, :, ROPE:], in_=bank[:, :, ROPE:])
            nc.sync.dma_start(out=out_rows[:, first : first + 2, Q_COLS : Q_COLS + HALF], in_=front[:])

        def kv_back(b, i):
            bank = bank_tile(b)
            kv_group(i, HALF, bank[:, 0:HALF])
            back = work.tile([P, HALF], F32, name="back", bufs=4)
            nc.scalar.copy(out=back[:], in_=bank[:, 0:HALF])
            nc.sync.dma_start(out=out_rows[:, i, Q_COLS + HALF :], in_=back[:])

        def q_pass(i, n, g, bank):
            j, k = divmod(QG * i + g, 2)
            nc.tensor.matmul_mx(
                out=bank[:],
                lhsT=qc[j][:, k, :].bitcast(FP8X4),
                lhsT_scale=qs[j][:, k, :],
                rhs=wb[n][:, g, :].bitcast(FP8X4),
                rhs_scale=sb[4 * g : P, BANK * n : BANK * (n + 1)],
                start=(g == 0),
                stop=(g == QG - 1),
            )

        def q_part(i, first, banks):
            n = len(banks)
            q = work.tile([P, n, BANK], F32, name="q%d" % n, bufs=4)
            sums = []
            for j, b in enumerate(banks):
                whole = bank_tile(b)
                for g in range(QG):
                    q_pass(i, first + j, g, whole)
                bank = whole[:].rearrange("p (b c) -> p b c", c=ROPE)
                blocks = q[:, j, :].rearrange("p (b c) -> p b c", c=ROPE)
                turning = (2 - 8 * (first + j)) % 3
                h = len(range(turning, 8, 3))
                terms = rope_terms(bank[:, turning::3, :], factors[:, i, :, :].unsqueeze(2).to_broadcast([P, 2, h, ROPE]))
                for r in range(3):
                    if r != turning:
                        nc.scalar.copy(out=blocks[:, r::3, :], in_=bank[:, r::3, :])
                sums.append((blocks[:, turning::3, :], terms))
            for target, terms in sums:
                rope_sum(target, terms)
            nc.sync.dma_start(
                out=out_rows[:, i, BANK * first : BANK * (first + n)], in_=q[:].rearrange("p j c -> p (j c)")
            )

        idle = bank_tile(7)
        keep_warm(idle, 4)
        cast_sorted(0, 0)
        cast_sorted(1, 0)
        for g in range(1, XG):
            cast_sorted(0, g)
            cast(1, g)
        turn(0, [(0, 0), (1, 0)])
        turn(1, [(0, 1), (1, 1)])
        keep_warm(idle, 1)
        turn(2, [(0, 2), (1, 2)])
        turn(3, [(0, 3), (1, 3)])
        widen(0, 0)
        for g in range(XG):
            cast(2, g)
            cast_sorted(3, g)
        turn(4, [(2, 0), (3, 0)])
        keep_warm(idle, 1)
        turn(5, [(2, 1), (3, 1)])
        turn(6, [(2, 2), (3, 2)])
        turn(7, [(2, 3), (3, 3)])
        for first, g in ((2, 0), (2, 1), (0, 2), (0, 3), (2, 2), (2, 3)):
            gather_x(first, g)
        for unit in PLANES:
            scale_planes(*unit)
        quant_x(0, 0, 1)
        widen(1, 0)
        widen(0, 1)
        quant_x(1, 0, 1)
        widen(1, 1)
        quant_x(0, 1, 1)
        quant_x(1, 1, 1)
        scale_x(2, 0)
        behind = (2, 0)
        for unit in [(2, 1)] + [(i, g) for g in (2, 3) for i in range(3)]:
            if unit in PLANES:
                weave(*unit)
            else:
                scale_x(*unit)
            quant_x(*behind, 1)
            behind = unit
        weave(3, 0)
        quant_x(2, 3, 1)
        weave(3, 1)
        weave(3, 2)
        quant_x(3, 0, 2)
        weave(3, 3)
        order_kv_scales()
        quant_x(3, 2, 2)
        order_kv_words()
        make_factors()
        banks = ((0, 5, 6), (4, 1, 7), (2, 3))
        for g, first, count in ((0, 0, 2), (1, 0, 2), (0, 2, 1), (1, 2, 1), (2, 0, 3), (3, 0, 2), (3, 2, 1)):
            for i in range(3):
                for n in range(first, first + count):
                    if i < 2 or (n < 2 and g >= 2):
                        qa_pass(i, g, n, banks[n][i])
            if (g, first) == (1, 2):
                for early in range(2):
                    for n in range(2):
                        qa_pass(2, early, n, banks[n][2])
        for i, n in ((0, 0), (0, 1), (1, 0), (1, 1), (2, 0), (2, 1), (0, 2), (1, 2)):
            round_qa(i, n)
        for g in range(XG):
            qa_pass(2, g, 2, 0)
        round_qa(2, 2)
        for n, b in enumerate((4, 5, 6)):
            for g in range(XG):
                qa_pass(3, g, n, b)
            round_qa(3, n)
        early = kv_fronts(1, 0)
        early_front, terms = rotate_fronts(early, 0)
        for j, b in enumerate((7, 2, 3, 0, 4, 5)):
            turn_qa(j, b)
        late = kv_fronts(6, 2)
        rope_sum(early_front[:, :, 0:ROPE], terms)
        for j in range(6):
            gather_qa(j)
            quant_qa(j)
            if j == 2:
                store_fronts(early, 0, early_front)
        late_front, terms = rotate_fronts(late, 2)
        rope_sum(late_front[:, :, 0:ROPE], terms)
        store_fronts(late, 2, late_front)
        ring = (7, 2, 3, 1, 0, 4, 5, 6)
        used = 0
        for first, count in ((0, 3), (4, 2), (3, 1)):
            for i in range(TILES):
                q_part(i, first, [ring[(used + j) % 8] for j in range(count)])
                used = used + count
        for i in range(TILES):
            kv_back(ring[i], i)
